import numpy as np
import ml_dtypes


def mxq(x, axis, fmt="e4m3"):
    dtype, down = {"e4m3": (ml_dtypes.float8_e4m3fn, 7), "e5m2": (ml_dtypes.float8_e5m2, 14)}[fmt]
    v = np.moveaxis(np.asarray(x, np.float32).astype(ml_dtypes.bfloat16).astype(np.float64), axis, -1)
    blocks = v.reshape(v.shape[:-1] + (-1, 32))
    amax = np.abs(blocks).max(-1, keepdims=True)
    byte = np.maximum(np.where(amax > 0, np.frexp(amax)[1] - 1 + 127, 0) - down, 1)
    scale = np.exp2(byte - 127.0)
    codes = (blocks / scale).astype(np.float32).astype(dtype).astype(np.float64)
    return np.moveaxis((codes * scale).reshape(v.shape), -1, axis)


WIDE = False


def mx_kscale(k):
    if not WIDE:
        return np.ones(k)
    levels = np.array([10, -10, 5, -5, 0])
    a = np.random.permutation(np.resize(levels, k // 512 * 4)).reshape(k // 512, 4)
    idx = np.arange(k)
    return np.exp2(a[idx // 512, idx % 128 // 32])


BF16 = ml_dtypes.bfloat16


def bf(x):
    return np.asarray(x, np.float32).astype(BF16)


def f64(x):
    return np.asarray(x).astype(np.float64)


N, F, H, O, D = 512, 512, 16, 128, 128


def setup_inputs():
    s = mx_kscale(F)
    keep = np.random.random((N, 1)) >= 0.1
    linked = np.random.random((N, 1)) >= 0.1
    edge = np.random.randint(0, 2, (1, N, N)) * linked
    return {"h": bf(np.random.standard_normal((1, N, F)) * keep * s),
            "a": bf(edge * (0.5 + np.random.random((1, N, N)))),
            "kernel": bf(np.random.standard_normal((H, F, O)) * 2.0 / np.sqrt(F) / s[:, None]),
            "f_self": bf(np.random.standard_normal((H, N, D)) * 1.2),
            "f_other": bf(np.random.standard_normal((H, N, D)) * 1.2)}


def reference(h, a, kernel, f_self, f_other):
    x = f64(h)[0]
    adj = f64(a)[0]
    feats = mxq(x, 1, "e4m3") @ mxq(f64(kernel), 1, "e4m3")
    dense = f64(f_self) @ f64(f_other).transpose(0, 2, 1)
    masked = adj[None] * dense
    masked = np.where(masked >= 0, masked, 0.2 * masked)
    masked = masked / np.sqrt(D)
    z = masked + np.where(adj == 0, -1e9, 0.0)[None]
    e = np.exp(z - z.max(-1, keepdims=True))
    den = e.sum(-1, keepdims=True)
    em = e * (adj != 0)[None]
    nf = (mxq(em, 2, "e4m3") @ mxq(feats, 1, "e4m3")) / den
    nf = np.maximum(nf, 0.0)
    row_mask = (np.sum((x != 0) * 1.0, axis=-1, keepdims=True) > 0) * 1.0
    nf = nf * row_mask[None]
    return nf.transpose(1, 0, 2).reshape(N, H * O)[None]

@@ -1,0 +1,270 @@
+import math
+from contextlib import ExitStack
+
+import concourse.mybir as mybir
+from concourse.masks import make_identity
+
+F32 = mybir.dt.float32
+BF16 = mybir.dt.bfloat16
+U32 = mybir.dt.uint32
+U8 = mybir.dt.uint8
+FP8X4 = mybir.dt.float8_e4m3fn_x4
+ALU = mybir.AluOpType
+ACT = mybir.ActivationFunctionType
+AXIS = mybir.AxisListType
+
+P = 128
+PACK = 4
+NODES = 512
+FEATS = 512
+HEADS = 16
+OUT = 128
+DIM = 128
+PAIR = 2
+LOAD_HEADS = 4
+
+LEAK = 0.2
+NO_EDGE = -(2.0**100)
+INV_SQRT_DIM = 1.0 / math.sqrt(DIM)
+
+FLOPS = 3 * 2 * HEADS * NODES * NODES * 128
+
+
+def block(i):
+    return slice(i * P, (i + 1) * P)
+
+
+def tile_gatlayersinglebatch_pa_t_kernel(tc, h, a, kernel, f_self, f_other, out):
+    nc = tc.nc
+    with ExitStack() as ctx:
+        const = ctx.enter_context(tc.tile_pool(name="const", bufs=1))
+        work = ctx.enter_context(tc.tile_pool(name="work", bufs=3))
+        psum = ctx.enter_context(tc.psum_pool(name="psum", bufs=1))
+
+        adj_sb = const.tile([P, PACK, NODES], BF16)
+        x_sb = const.tile([P, PACK, FEATS], BF16)
+        fs_sb = const.tile([P, HEADS, PACK, DIM], BF16)
+        fo_sb = const.tile([P, HEADS, PACK, DIM], BF16)
+        w_sb = const.tile([P, HEADS, PACK, OUT], BF16)
+        nc.sync.dma_start(out=adj_sb[:], in_=a.rearrange("b (p j) m -> p (b j) m", j=PACK))
+        for first in range(0, HEADS, LOAD_HEADS):
+            heads = slice(first, first + LOAD_HEADS)
+            nc.sync.dma_start(
+                out=fs_sb[:, heads], in_=f_self[heads].rearrange("i (p j) d -> p i j d", j=PACK)
+            )
+            nc.sync.dma_start(
+                out=fo_sb[:, heads], in_=f_other[heads].rearrange("i (p j) d -> p i j d", j=PACK)
+            )
+            if first == 0:
+                nc.sync.dma_start(out=x_sb[:], in_=h.rearrange("b (p j) f -> p (b j) f", j=PACK))
+            nc.sync.dma_start(
+                out=w_sb[:, heads], in_=kernel[heads].rearrange("i (p j) o -> p i j o", j=PACK)
+            )
+        out_rows = out.rearrange("b (p j) c -> p (b j) c", j=PACK)
+
+        ident_bf = const.tile([P, P], BF16)
+        make_identity(nc, ident_bf[:])
+        ident_f32 = const.tile([P, P], F32)
+        make_identity(nc, ident_f32[:])
+
+        no_edge = const.tile([P, PACK, PACK, P], BF16)
+        n_no_edge = const.tile([P, PACK], F32)
+        weight = const.tile([P, PACK, PACK, P], F32)
+        no_edge_T = const.tile([P, PACK, PACK, P], F32)
+        adj_tq = adj_sb[:].rearrange("p j (q t) -> p j t q", t=PACK)
+        for j in range(PACK):
+            nc.vector.tensor_scalar(
+                out=no_edge[:, j],
+                in0=adj_tq[:, j],
+                scalar1=0.0,
+                scalar2=None,
+                op0=ALU.is_equal,
+                op1=ALU.add,
+                accum_out=n_no_edge[:, j : j + 1],
+            )
+            nc.vector.scalar_tensor_tensor(
+                out=weight[:, j],
+                in0=adj_tq[:, j],
+                scalar=INV_SQRT_DIM,
+                in1=no_edge[:, j],
+                op0=ALU.mult,
+                op1=ALU.add,
+            )
+            no_edge_ps = psum.tile([P, PACK, P], BF16, tag="fT")
+            for t in range(PACK):
+                nc.tensor.transpose(no_edge_ps[:, t, :], no_edge[:, j, t, :], ident_bf[:])
+            nc.scalar.mul(out=no_edge_T[:, j], in_=no_edge_ps[:], mul=NO_EDGE)
+
+        x_words = x_sb[:].bitcast(F32).rearrange("p t (w u) -> p t u w", u=2)
+        x_grouped = const.tile([P, PACK, P, PACK], BF16, align_bytes=64)
+        x_grouped_words = x_grouped[:].bitcast(F32)
+        for first in range(0, PACK, PAIR):
+            xT_ps = psum.tile([P, PAIR, 2, P], F32, tag="feat")
+            for t in range(PAIR):
+                for u in range(2):
+                    nc.tensor.transpose(xT_ps[:, t, u, :], x_words[:, first + t, u, :], ident_f32[:])
+            nc.scalar.copy(
+                out=x_grouped_words[:, first : first + PAIR], in_=xT_ps[:].rearrange("p t u q -> p t q u")
+            )
+        x_codes = const.tile([P, NODES], U32, align_bytes=64)
+        x_scales = const.tile([P, NODES], U8, align_bytes=64)
+        nc.vector.quantize_mx(
+            out=x_codes[:].bitcast(FP8X4),
+            scales=x_scales[:],
+            in_=x_grouped[:].rearrange("p t q s -> p (t q s)"),
+        )
+
+        is_feature = const.tile([P, PACK, FEATS], BF16)
+        n_feature = const.tile([P, PACK], F32)
+        for j in range(PACK):
+            nc.vector.tensor_scalar(
+                out=is_feature[:, j],
+                in0=x_sb[:, j],
+                scalar1=0.0,
+                scalar2=None,
+                op0=ALU.not_equal,
+                op1=ALU.add,
+                accum_out=n_feature[:, j : j + 1],
+            )
+        has_feature = const.tile([P, PACK], F32)
+        nc.vector.tensor_single_scalar(out=has_feature[:], in_=n_feature[:], scalar=0.0, op=ALU.is_gt)
+        keep = const.tile([P, PACK], F32)
+        nc.vector.scalar_tensor_tensor(
+            out=keep[:],
+            in0=n_no_edge[:],
+            scalar=float(NODES),
+            in1=has_feature[:],
+            op0=ALU.is_lt,
+            op1=ALU.mult,
+        )
+
+        feat_codes = const.tile([P, HEADS * OUT], U32, align_bytes=64)
+        feat_scales = const.tile([P, HEADS * OUT], U8, align_bytes=64)
+
+        def project(i):
+            w_grouped = work.tile([P, OUT, PACK], BF16, align_bytes=64)
+            nc.scalar.copy(out=w_grouped[:], in_=w_sb[:, i].rearrange("p j o -> p o j"))
+            w_codes = work.tile([P, OUT], U32, align_bytes=64)
+            w_scales = work.tile([P, OUT], U8, align_bytes=64)
+            nc.vector.quantize_mx(
+                out=w_codes[:].bitcast(FP8X4),
+                scales=w_scales[:],
+                in_=w_grouped[:].rearrange("p o j -> p (o j)"),
+            )
+            feat_ps = psum.tile([P, PACK, OUT], F32, tag="feat")
+            for t in range(PACK):
+                nc.tensor.matmul_mx(
+                    out=feat_ps[:, t, :],
+                    lhsT=x_codes[:, block(t)].bitcast(FP8X4),
+                    lhsT_scale=x_scales[:, block(t)],
+                    rhs=w_codes[:].bitcast(FP8X4),
+                    rhs_scale=w_scales[:],
+                    start=True,
+                    stop=True,
+                )
+            feat_grouped = work.tile([P, OUT, PACK], BF16, align_bytes=64)
+            nc.scalar.copy(out=feat_grouped[:], in_=feat_ps[:].rearrange("q t o -> q o t"))
+            nc.vector.quantize_mx(
+                out=feat_codes[:, block(i)].bitcast(FP8X4),
+                scales=feat_scales[:, block(i)],
+                in_=feat_grouped[:].rearrange("q o t -> q (o t)"),
+            )
+
+        def transpose_attention_features(i):
+            fT_ps = psum.tile([P, 2, PACK, P], BF16, tag="fT")
+            for j in range(PACK):
+                nc.tensor.transpose(fT_ps[:, 0, j, :], fs_sb[:, i, j, :], ident_bf[:])
+            for t in range(PACK):
+                nc.tensor.transpose(fT_ps[:, 1, t, :], fo_sb[:, i, t, :], ident_bf[:])
+            fT = work.tile([P, 2, NODES], BF16)
+            nc.scalar.copy(out=fT[:], in_=fT_ps[:].rearrange("d s j p -> d s (j p)"))
+            return fT
+
+        def attention_weights(fT, first, den):
+            z = work.tile([P, PAIR, NODES], F32)
+            for u in range(PAIR):
+                dense_ps = psum.tile([P, NODES], F32, tag="dense", bufs=3)
+                nc.tensor.matmul(
+                    out=dense_ps[:], lhsT=fT[:, 0, block(first + u)], rhs=fT[:, 1, :], start=True, stop=False
+                )
+                for t in range(PACK):
+                    nc.tensor.matmul(
+                        out=dense_ps[:, block(t)],
+                        lhsT=no_edge_T[:, first + u, t, :],
+                        rhs=ident_f32[:],
+                        is_transpose=True,
+                        start=False,
+                        stop=(t == PACK - 1),
+                    )
+                nc.vector.tensor_tensor(
+                    out=z[:, u, :],
+                    in0=dense_ps[:],
+                    in1=weight[:, first + u].rearrange("p t q -> p (t q)"),
+                    op=ALU.mult,
+                )
+            z_flat = z[:].rearrange("p u m -> p (u m)")
+            nc.vector.scalar_tensor_tensor(
+                out=z_flat, in0=z_flat, scalar=LEAK, in1=z_flat, op0=ALU.mult, op1=ALU.max
+            )
+            neg_max = work.tile([P, PAIR], F32)
+            nc.vector.tensor_reduce(out=neg_max[:], in_=z[:], axis=AXIS.X, op=ALU.max, negate=True)
+            em = work.tile([P, PAIR, NODES], BF16)
+            for u in range(PAIR):
+                nc.scalar.activation(
+                    out=em[:, u, :],
+                    in_=z[:, u, :],
+                    func=ACT.Exp,
+                    bias=neg_max[:, u : u + 1],
+                    scale=1.0,
+                    accum_out=den[:, first + u : first + u + 1],
+                )
+            return em
+
+        def aggregate(i, first, em, row_scale, result):
+            emT_ps = psum.tile([P, PAIR, PACK, P], BF16, tag="emT", bufs=2)
+            for u in range(PAIR):
+                for t in range(PACK):
+                    nc.tensor.transpose(emT_ps[:, u, t, :], em[:, u, block(t)], ident_bf[:])
+            em_grouped = work.tile([P, PAIR, P, PACK], BF16, align_bytes=64)
+            nc.scalar.copy(out=em_grouped[:], in_=emT_ps[:].rearrange("q u t n -> q u n t"))
+            em_codes = work.tile([P, PAIR * P], U32, align_bytes=64)
+            em_scales = work.tile([P, PAIR * P], U8, align_bytes=64)
+            nc.vector.quantize_mx(
+                out=em_codes[:].bitcast(FP8X4),
+                scales=em_scales[:],
+                in_=em_grouped[:].rearrange("q u n t -> q (u n t)"),
+            )
+            sum_ps = psum.tile([P, PAIR, OUT], F32, tag="sum")
+            for u in range(PAIR):
+                nc.tensor.matmul_mx(
+                    out=sum_ps[:, u, :],
+                    lhsT=em_codes[:, block(u)].bitcast(FP8X4),
+                    lhsT_scale=em_scales[:, block(u)],
+                    rhs=feat_codes[:, block(i)].bitcast(FP8X4),
+                    rhs_scale=feat_scales[:, block(i)],
+                    start=True,
+                    stop=True,
+                )
+                nc.scalar.activation(
+                    out=result[:, first + u, :],
+                    in_=sum_ps[:, u, :],
+                    func=ACT.Relu,
+                    scale=row_scale[:, first + u : first + u + 1],
+                )
+
+        fT_next = transpose_attention_features(0)
+        project(0)
+        for i in range(HEADS):
+            fT = fT_next
+            if i + 1 < HEADS:
+                fT_next = transpose_attention_features(i + 1)
+                project(i + 1)
+            den = work.tile([P, PACK], F32)
+            ems = [attention_weights(fT, first, den) for first in range(0, PACK, PAIR)]
+            row_scale = work.tile([P, PACK], F32)
+            nc.vector.reciprocal(out=row_scale[:], in_=den[:])
+            nc.vector.tensor_mul(out=row_scale[:], in0=row_scale[:], in1=keep[:])
+            result = work.tile([P, PACK, OUT], F32)
+            for first, em in zip(range(0, PACK, PAIR), ems):
+                aggregate(i, first, em, row_scale, result)
+            nc.sync.dma_start(out=out_rows[:, :, block(i)], in_=result[:])

@@ -15,12 +15,16 @@ AXIS = mybir.AxisListType
 
 P = 128
 PACK = 4
+HALF = 2
 NODES = 512
 FEATS = 512
 HEADS = 16
 OUT = 128
 DIM = 128
 PAIR = 2
+UNITS = HEADS * PACK
+PAIRS = UNITS // PAIR
+PAIRS_PER_HEAD = PACK // PAIR
 LOAD_HEADS = 4
 
 LEAK = 0.2
@@ -37,6 +41,7 @@ def block(i):
 def tile_gatlayersinglebatch_pa_t_kernel(tc, h, a, kernel, f_self, f_other, out):
     nc = tc.nc
     with ExitStack() as ctx:
+        ctx.enter_context(tc.manual_schedule())
         const = ctx.enter_context(tc.tile_pool(name="const", bufs=1))
         work = ctx.enter_context(tc.tile_pool(name="work", bufs=3))
         psum = ctx.enter_context(tc.psum_pool(name="psum", bufs=1))
@@ -67,52 +72,75 @@ def tile_gatlayersinglebatch_pa_t_kernel(tc, h, a, kernel, f_self, f_other, out)
         ident_f32 = const.tile([P, P], F32)
         make_identity(nc, ident_f32[:])
 
-        no_edge = const.tile([P, PACK, PACK, P], BF16)
+        fT_ps_of = {}
+        fT_of = {}
+
+        def transpose_f(i):
+            if not 0 <= i < HEADS:
+                return
+            fT_ps = psum.tile([P, 2, PACK, P], BF16, tag="fT")
+            for j in range(PACK):
+                nc.tensor.transpose(fT_ps[:, 0, j, :], fs_sb[:, i, j, :], ident_bf[:])
+            for t in range(PACK):
+                nc.tensor.transpose(fT_ps[:, 1, t, :], fo_sb[:, i, t, :], ident_bf[:])
+            fT_ps_of[i] = fT_ps
+
+        def copy_f(i):
+            if not 0 <= i < HEADS:
+                return
+            fT = work.tile([P, 2, NODES], BF16)
+            nc.scalar.copy(out=fT[:, 0, :], in_=fT_ps_of[i][:, 0].rearrange("d j p -> d (j p)"))
+            nc.scalar.copy(
+                out=fT[:, 1, :].rearrange("d (u q e) -> d u q e", u=HALF, e=HALF),
+                in_=fT_ps_of[i][:, 1].rearrange("d (u e) q -> d u q e", e=HALF),
+            )
+            fT_of[i] = fT
+
+        transpose_f(0)
+        copy_f(0)
+
+        x_words = x_sb[:].bitcast(F32).rearrange("p t (w u) -> p t u w", u=HALF)
+        x_grouped = const.tile([P, PACK, P, PACK], BF16, align_bytes=64)
+        x_grouped_words = x_grouped[:].bitcast(F32)
+        for first in range(0, PACK, PAIR):
+            xT_ps = psum.tile([P, PAIR, HALF, P], F32, tag="dense", bufs=3)
+            for t in range(PAIR):
+                for u in range(HALF):
+                    nc.tensor.transpose(xT_ps[:, t, u, :], x_words[:, first + t, u, :], ident_f32[:])
+            nc.scalar.copy(
+                out=x_grouped_words[:, first : first + PAIR], in_=xT_ps[:].rearrange("p t u q -> p t q u")
+            )
+
+        no_edge = const.tile([P, PACK, NODES], BF16)
         n_no_edge = const.tile([P, PACK], F32)
-        weight = const.tile([P, PACK, PACK, P], F32)
+        weight = const.tile([P, PACK, NODES], F32)
         no_edge_T = const.tile([P, PACK, PACK, P], F32)
-        adj_tq = adj_sb[:].rearrange("p j (q t) -> p j t q", t=PACK)
+        adj_uqe = adj_sb[:].rearrange("p j (q u e) -> p j u q e", u=HALF, e=HALF)
+        no_edge_uqe = no_edge[:].rearrange("p j (u q e) -> p j u q e", u=HALF, e=HALF)
+        weight_uqe = weight[:].rearrange("p j (u q e) -> p j u q e", u=HALF, e=HALF)
         for j in range(PACK):
             nc.vector.tensor_scalar(
-                out=no_edge[:, j],
-                in0=adj_tq[:, j],
+                out=no_edge_uqe[:, j],
+                in0=adj_uqe[:, j],
                 scalar1=0.0,
                 scalar2=None,
                 op0=ALU.is_equal,
                 op1=ALU.add,
                 accum_out=n_no_edge[:, j : j + 1],
             )
-            nc.vector.scalar_tensor_tensor(
-                out=weight[:, j],
-                in0=adj_tq[:, j],
-                scalar=INV_SQRT_DIM,
-                in1=no_edge[:, j],
-                op0=ALU.mult,
-                op1=ALU.add,
-            )
-            no_edge_ps = psum.tile([P, PACK, P], BF16, tag="fT")
-            for t in range(PACK):
-                nc.tensor.transpose(no_edge_ps[:, t, :], no_edge[:, j, t, :], ident_bf[:])
+            for u in range(HALF):
+                nc.vector.scalar_tensor_tensor(
+                    out=weight_uqe[:, j, u],
+                    in0=adj_uqe[:, j, u],
+                    scalar=INV_SQRT_DIM,
+                    in1=no_edge_uqe[:, j, u],
+                    op0=ALU.mult,
+                    op1=ALU.add,
+                )
+            no_edge_ps = psum.tile([P, PACK, P], BF16, tag="emT", bufs=2)
+            for b in range(PACK):
+                nc.tensor.transpose(no_edge_ps[:, b, :], no_edge[:, j, block(b)], ident_bf[:])
             nc.scalar.mul(out=no_edge_T[:, j], in_=no_edge_ps[:], mul=NO_EDGE)
-
-        x_words = x_sb[:].bitcast(F32).rearrange("p t (w u) -> p t u w", u=2)
-        x_grouped = const.tile([P, PACK, P, PACK], BF16, align_bytes=64)
-        x_grouped_words = x_grouped[:].bitcast(F32)
-        for first in range(0, PACK, PAIR):
-            xT_ps = psum.tile([P, PAIR, 2, P], F32, tag="feat")
-            for t in range(PAIR):
-                for u in range(2):
-                    nc.tensor.transpose(xT_ps[:, t, u, :], x_words[:, first + t, u, :], ident_f32[:])
-            nc.scalar.copy(
-                out=x_grouped_words[:, first : first + PAIR], in_=xT_ps[:].rearrange("p t u q -> p t q u")
-            )
-        x_codes = const.tile([P, NODES], U32, align_bytes=64)
-        x_scales = const.tile([P, NODES], U8, align_bytes=64)
-        nc.vector.quantize_mx(
-            out=x_codes[:].bitcast(FP8X4),
-            scales=x_scales[:],
-            in_=x_grouped[:].rearrange("p t q s -> p (t q s)"),
-        )
 
         is_feature = const.tile([P, PACK, FEATS], BF16)
         n_feature = const.tile([P, PACK], F32)
@@ -138,19 +166,44 @@ def tile_gatlayersinglebatch_pa_t_kernel(tc, h, a, kernel, f_self, f_other, out)
             op1=ALU.mult,
         )
 
+        x_codes = const.tile([P, NODES], U32, align_bytes=64)
+        x_scales = const.tile([P, NODES], U8, align_bytes=64)
+        nc.vector.quantize_mx(
+            out=x_codes[:].bitcast(FP8X4),
+            scales=x_scales[:],
+            in_=x_grouped[:].rearrange("p t q s -> p (t q s)"),
+        )
+
+        w_grouped_of = {}
+        w_mx_of = {}
+        feat_ps_of = {}
+        feat_grouped_of = {}
         feat_codes = const.tile([P, HEADS * OUT], U32, align_bytes=64)
         feat_scales = const.tile([P, HEADS * OUT], U8, align_bytes=64)
 
-        def project(i):
+        def regroup_w(i):
+            if not 0 <= i < HEADS:
+                return
             w_grouped = work.tile([P, OUT, PACK], BF16, align_bytes=64)
             nc.scalar.copy(out=w_grouped[:], in_=w_sb[:, i].rearrange("p j o -> p o j"))
+            w_grouped_of[i] = w_grouped
+
+        def quantise_w(i):
+            if not 0 <= i < HEADS:
+                return
             w_codes = work.tile([P, OUT], U32, align_bytes=64)
             w_scales = work.tile([P, OUT], U8, align_bytes=64)
             nc.vector.quantize_mx(
                 out=w_codes[:].bitcast(FP8X4),
                 scales=w_scales[:],
-                in_=w_grouped[:].rearrange("p o j -> p (o j)"),
+                in_=w_grouped_of[i][:].rearrange("p o j -> p (o j)"),
             )
+            w_mx_of[i] = (w_codes, w_scales)
+
+        def project(i):
+            if not 0 <= i < HEADS:
+                return
+            w_codes, w_scales = w_mx_of[i]
             feat_ps = psum.tile([P, PACK, OUT], F32, tag="feat")
             for t in range(PACK):
                 nc.tensor.matmul_mx(
@@ -162,109 +215,195 @@ def tile_gatlayersinglebatch_pa_t_kernel(tc, h, a, kernel, f_self, f_other, out)
                     start=True,
                     stop=True,
                 )
+            feat_ps_of[i] = feat_ps
+
+        def regroup_feats(i):
+            if not 0 <= i < HEADS:
+                return
             feat_grouped = work.tile([P, OUT, PACK], BF16, align_bytes=64)
-            nc.scalar.copy(out=feat_grouped[:], in_=feat_ps[:].rearrange("q t o -> q o t"))
+            nc.scalar.copy(out=feat_grouped[:], in_=feat_ps_of[i][:].rearrange("q t o -> q o t"))
+            feat_grouped_of[i] = feat_grouped
+
+        def quantise_feats(i):
+            if not 0 <= i < HEADS:
+                return
             nc.vector.quantize_mx(
                 out=feat_codes[:, block(i)].bitcast(FP8X4),
                 scales=feat_scales[:, block(i)],
-                in_=feat_grouped[:].rearrange("q o t -> q (o t)"),
+                in_=feat_grouped_of[i][:].rearrange("q o t -> q (o t)"),
             )
 
-        def transpose_attention_features(i):
-            fT_ps = psum.tile([P, 2, PACK, P], BF16, tag="fT")
-            for j in range(PACK):
-                nc.tensor.transpose(fT_ps[:, 0, j, :], fs_sb[:, i, j, :], ident_bf[:])
-            for t in range(PACK):
-                nc.tensor.transpose(fT_ps[:, 1, t, :], fo_sb[:, i, t, :], ident_bf[:])
-            fT = work.tile([P, 2, NODES], BF16)
-            nc.scalar.copy(out=fT[:], in_=fT_ps[:].rearrange("d s j p -> d s (j p)"))
-            return fT
+        dense_of = {}
+        z_of = {}
+        neg_max_of = {}
+        em_of = {}
+        den_of = {}
+        row_scale_of = {}
+        emT_of = {}
+        em_grouped_of = {}
+        em_mx_of = {}
+        sum_of = {}
+        result_of = {}
 
-        def attention_weights(fT, first, den):
-            z = work.tile([P, PAIR, NODES], F32)
-            for u in range(PAIR):
-                dense_ps = psum.tile([P, NODES], F32, tag="dense", bufs=3)
+        def score(g):
+            if not 0 <= g < UNITS:
+                return
+            fT = fT_of[g // PACK]
+            j = g % PACK
+            dense_ps = psum.tile([P, NODES], F32, tag="dense", bufs=3)
+            nc.tensor.matmul(out=dense_ps[:], lhsT=fT[:, 0, block(j)], rhs=fT[:, 1, :], start=True, stop=False)
+            for b in range(PACK):
                 nc.tensor.matmul(
-                    out=dense_ps[:], lhsT=fT[:, 0, block(first + u)], rhs=fT[:, 1, :], start=True, stop=False
+                    out=dense_ps[:, block(b)],
+                    lhsT=no_edge_T[:, j, b, :],
+                    rhs=ident_f32[:],
+                    is_transpose=True,
+                    start=False,
+                    stop=(b == PACK - 1),
                 )
-                for t in range(PACK):
-                    nc.tensor.matmul(
-                        out=dense_ps[:, block(t)],
-                        lhsT=no_edge_T[:, first + u, t, :],
-                        rhs=ident_f32[:],
-                        is_transpose=True,
-                        start=False,
-                        stop=(t == PACK - 1),
-                    )
-                nc.vector.tensor_tensor(
-                    out=z[:, u, :],
-                    in0=dense_ps[:],
-                    in1=weight[:, first + u].rearrange("p t q -> p (t q)"),
-                    op=ALU.mult,
-                )
-            z_flat = z[:].rearrange("p u m -> p (u m)")
+            dense_of[g] = dense_ps
+
+        def weigh(g):
+            if not 0 <= g < UNITS:
+                return
+            if g % PAIR == 0:
+                z = work.tile([P, PAIR, NODES], F32)
+                z_of[g // PAIR] = z
+            nc.vector.tensor_tensor(
+                out=z_of[g // PAIR][:, g % PAIR, :], in0=dense_of[g][:], in1=weight[:, g % PACK, :], op=ALU.mult
+            )
+
+        def leak(k):
+            if not 0 <= k < PAIRS:
+                return
+            z_flat = z_of[k][:].rearrange("p v m -> p (v m)")
             nc.vector.scalar_tensor_tensor(
                 out=z_flat, in0=z_flat, scalar=LEAK, in1=z_flat, op0=ALU.mult, op1=ALU.max
             )
-            neg_max = work.tile([P, PAIR], F32)
-            nc.vector.tensor_reduce(out=neg_max[:], in_=z[:], axis=AXIS.X, op=ALU.max, negate=True)
-            em = work.tile([P, PAIR, NODES], BF16)
-            for u in range(PAIR):
-                nc.scalar.activation(
-                    out=em[:, u, :],
-                    in_=z[:, u, :],
-                    func=ACT.Exp,
-                    bias=neg_max[:, u : u + 1],
-                    scale=1.0,
-                    accum_out=den[:, first + u : first + u + 1],
-                )
-            return em
 
-        def aggregate(i, first, em, row_scale, result):
-            emT_ps = psum.tile([P, PAIR, PACK, P], BF16, tag="emT", bufs=2)
-            for u in range(PAIR):
-                for t in range(PACK):
-                    nc.tensor.transpose(emT_ps[:, u, t, :], em[:, u, block(t)], ident_bf[:])
+        def row_max(k):
+            if not 0 <= k < PAIRS:
+                return
+            neg_max = work.tile([P, PAIR], F32)
+            nc.vector.tensor_reduce(out=neg_max[:], in_=z_of[k][:], axis=AXIS.X, op=ALU.max, negate=True)
+            neg_max_of[k] = neg_max
+
+        def exponentials(k):
+            if not 0 <= k < PAIRS:
+                return
+            if k % PAIRS_PER_HEAD == 0:
+                den = work.tile([P, PACK], F32)
+                den_of[k // PAIRS_PER_HEAD] = den
+            em = work.tile([P, PAIR, NODES], BF16)
+            for v in range(PAIR):
+                j = (PAIR * k + v) % PACK
+                nc.scalar.activation(
+                    out=em[:, v, :],
+                    in_=z_of[k][:, v, :],
+                    func=ACT.Exp,
+                    bias=neg_max_of[k][:, v : v + 1],
+                    scale=1.0,
+                    accum_out=den_of[k // PAIRS_PER_HEAD][:, j : j + 1],
+                )
+            em_of[k] = em
+
+        def row_scales(i):
+            if not 0 <= i < HEADS:
+                return
+            row_scale = work.tile([P, PACK], F32)
+            nc.vector.reciprocal(out=row_scale[:], in_=den_of[i][:])
+            nc.vector.tensor_mul(out=row_scale[:], in0=row_scale[:], in1=keep[:])
+            row_scale_of[i] = row_scale
+
+        def transpose_em(k):
+            if not 0 <= k < PAIRS:
+                return
+            em_words = em_of[k][:].bitcast(F32)
+            emT_ps = psum.tile([P, PAIR, HALF, P], F32, tag="emT", bufs=2)
+            for v in range(PAIR):
+                for u in range(HALF):
+                    nc.tensor.transpose(emT_ps[:, v, u, :], em_words[:, v, block(u)], ident_f32[:])
+            emT_of[k] = emT_ps
+
+        def regroup_em(k):
+            if not 0 <= k < PAIRS:
+                return
             em_grouped = work.tile([P, PAIR, P, PACK], BF16, align_bytes=64)
-            nc.scalar.copy(out=em_grouped[:], in_=emT_ps[:].rearrange("q u t n -> q u n t"))
+            nc.scalar.copy(out=em_grouped[:].bitcast(F32), in_=emT_of[k][:].rearrange("q v u n -> q v n u"))
+            em_grouped_of[k] = em_grouped
+
+        def quantise_em(k):
+            if not 0 <= k < PAIRS:
+                return
             em_codes = work.tile([P, PAIR * P], U32, align_bytes=64)
             em_scales = work.tile([P, PAIR * P], U8, align_bytes=64)
             nc.vector.quantize_mx(
                 out=em_codes[:].bitcast(FP8X4),
                 scales=em_scales[:],
-                in_=em_grouped[:].rearrange("q u n t -> q (u n t)"),
+                in_=em_grouped_of[k][:].rearrange("q v n s -> q (v n s)"),
             )
+            em_mx_of[k] = (em_codes, em_scales)
+
+        def multiply(k):
+            if not 0 <= k < PAIRS:
+                return
+            em_codes, em_scales = em_mx_of[k]
+            i = k // PAIRS_PER_HEAD
             sum_ps = psum.tile([P, PAIR, OUT], F32, tag="sum")
-            for u in range(PAIR):
+            for v in range(PAIR):
                 nc.tensor.matmul_mx(
-                    out=sum_ps[:, u, :],
-                    lhsT=em_codes[:, block(u)].bitcast(FP8X4),
-                    lhsT_scale=em_scales[:, block(u)],
+                    out=sum_ps[:, v, :],
+                    lhsT=em_codes[:, block(v)].bitcast(FP8X4),
+                    lhsT_scale=em_scales[:, block(v)],
                     rhs=feat_codes[:, block(i)].bitcast(FP8X4),
                     rhs_scale=feat_scales[:, block(i)],
                     start=True,
                     stop=True,
                 )
-                nc.scalar.activation(
-                    out=result[:, first + u, :],
-                    in_=sum_ps[:, u, :],
-                    func=ACT.Relu,
-                    scale=row_scale[:, first + u : first + u + 1],
-                )
+            sum_of[k] = sum_ps
 
-        fT_next = transpose_attention_features(0)
-        project(0)
-        for i in range(HEADS):
-            fT = fT_next
-            if i + 1 < HEADS:
-                fT_next = transpose_attention_features(i + 1)
+        def finish(k):
+            if not 0 <= k < PAIRS:
+                return
+            i = k // PAIRS_PER_HEAD
+            if k % PAIRS_PER_HEAD == 0:
+                result = work.tile([P, PACK, OUT], F32)
+                result_of[i] = result
+            for v in range(PAIR):
+                j = (PAIR * k + v) % PACK
+                nc.scalar.activation(
+                    out=result_of[i][:, j, :],
+                    in_=sum_of[k][:, v, :],
+                    func=ACT.Relu,
+                    scale=row_scale_of[i][:, j : j + 1],
+                )
+            if k % PAIRS_PER_HEAD == PAIRS_PER_HEAD - 1:
+                nc.sync.dma_start(out=out_rows[:, :, block(i)], in_=result_of[i][:])
+
+        for k in range(-2, PAIRS + 3):
+            i = k // PAIRS_PER_HEAD
+            first_of_head = k % PAIRS_PER_HEAD == 0
+            score(PAIR * k + 4)
+            exponentials(k - 1)
+            leak(k)
+            weigh(PAIR * k + 2)
+            multiply(k - 3)
+            if first_of_head:
+                regroup_em(k - 2)
+            else:
                 project(i + 1)
-            den = work.tile([P, PACK], F32)
-            ems = [attention_weights(fT, first, den) for first in range(0, PACK, PAIR)]
-            row_scale = work.tile([P, PACK], F32)
-            nc.vector.reciprocal(out=row_scale[:], in_=den[:])
-            nc.vector.tensor_mul(out=row_scale[:], in0=row_scale[:], in1=keep[:])
-            result = work.tile([P, PACK, OUT], F32)
-            for first, em in zip(range(0, PACK, PAIR), ems):
-                aggregate(i, first, em, row_scale, result)
-            nc.sync.dma_start(out=out_rows[:, :, block(i)], in_=result[:])
+                copy_f(i + 2)
+                regroup_em(k - 2)
+            transpose_em(k - 1)
+            score(PAIR * k + 5)
+            row_max(k)
+            weigh(PAIR * k + 3)
+            finish(k - 3)
+            quantise_em(k - 2)
+            if first_of_head:
+                row_scales(i - 1)
+                transpose_f(i + 2)
+                regroup_w(i + 1)
+                quantise_w(i + 1)
+                regroup_feats(i)
+                quantise_feats(i)

@@ -41,7 +41,6 @@ def block(i):
 def tile_gatlayersinglebatch_pa_t_kernel(tc, h, a, kernel, f_self, f_other, out):
     nc = tc.nc
     with ExitStack() as ctx:
-        ctx.enter_context(tc.manual_schedule())
         const = ctx.enter_context(tc.tile_pool(name="const", bufs=1))
         work = ctx.enter_context(tc.tile_pool(name="work", bufs=3))
         psum = ctx.enter_context(tc.psum_pool(name="psum", bufs=1))

@@ -29,7 +29,8 @@ LOAD_HEADS = 4
 
 LEAK = 0.2
 NO_EDGE = -(2.0**100)
-INV_SQRT_DIM = 1.0 / math.sqrt(DIM)
+LEAK_OVER_SQRT_DIM = LEAK / math.sqrt(DIM)
+RISE = 1.0 / LEAK - 1.0
 
 FLOPS = 3 * 2 * HEADS * NODES * NODES * 128
 
@@ -50,20 +51,34 @@ def tile_gatlayersinglebatch_pa_t_kernel(tc, h, a, kernel, f_self, f_other, out)
         fs_sb = const.tile([P, HEADS, PACK, DIM], BF16)
         fo_sb = const.tile([P, HEADS, PACK, DIM], BF16)
         w_sb = const.tile([P, HEADS, PACK, OUT], BF16)
-        nc.sync.dma_start(out=adj_sb[:], in_=a.rearrange("b (p j) m -> p (b j) m", j=PACK))
-        for first in range(0, HEADS, LOAD_HEADS):
-            heads = slice(first, first + LOAD_HEADS)
+        adj_rows = a.rearrange("b (p j) m -> p (b j) m", j=PACK)
+
+        def load_adj(j):
+            nc.sync.dma_start(out=adj_sb[:, j], in_=adj_rows[:, j])
+
+        def load_f(heads):
             nc.sync.dma_start(
                 out=fs_sb[:, heads], in_=f_self[heads].rearrange("i (p j) d -> p i j d", j=PACK)
             )
             nc.sync.dma_start(
                 out=fo_sb[:, heads], in_=f_other[heads].rearrange("i (p j) d -> p i j d", j=PACK)
             )
-            if first == 0:
-                nc.sync.dma_start(out=x_sb[:], in_=h.rearrange("b (p j) f -> p (b j) f", j=PACK))
+
+        def load_w(heads):
             nc.sync.dma_start(
                 out=w_sb[:, heads], in_=kernel[heads].rearrange("i (p j) o -> p i j o", j=PACK)
             )
+
+        load_adj(0)
+        load_f(slice(0, 1))
+        for j in range(1, PACK):
+            load_adj(j)
+        nc.sync.dma_start(out=x_sb[:], in_=h.rearrange("b (p j) f -> p (b j) f", j=PACK))
+        load_f(slice(1, LOAD_HEADS))
+        load_w(slice(0, LOAD_HEADS))
+        for first in range(LOAD_HEADS, HEADS, LOAD_HEADS):
+            load_f(slice(first, first + LOAD_HEADS))
+            load_w(slice(first, first + LOAD_HEADS))
         out_rows = out.rearrange("b (p j) c -> p (b j) c", j=PACK)
 
         ident_bf = const.tile([P, P], BF16)
@@ -98,80 +113,72 @@ def tile_gatlayersinglebatch_pa_t_kernel(tc, h, a, kernel, f_self, f_other, out)
         transpose_f(0)
         copy_f(0)
 
-        x_words = x_sb[:].bitcast(F32).rearrange("p t (w u) -> p t u w", u=HALF)
-        x_grouped = const.tile([P, PACK, P, PACK], BF16, align_bytes=64)
-        x_grouped_words = x_grouped[:].bitcast(F32)
-        for first in range(0, PACK, PAIR):
-            xT_ps = psum.tile([P, PAIR, HALF, P], F32, tag="dense", bufs=3)
-            for t in range(PAIR):
-                for u in range(HALF):
-                    nc.tensor.transpose(xT_ps[:, t, u, :], x_words[:, first + t, u, :], ident_f32[:])
-            nc.scalar.copy(
-                out=x_grouped_words[:, first : first + PAIR], in_=xT_ps[:].rearrange("p t u q -> p t q u")
-            )
-
         no_edge = const.tile([P, PACK, NODES], BF16)
-        n_no_edge = const.tile([P, PACK], F32)
         weight = const.tile([P, PACK, NODES], F32)
         no_edge_T = const.tile([P, PACK, PACK, P], F32)
         adj_uqe = adj_sb[:].rearrange("p j (q u e) -> p j u q e", u=HALF, e=HALF)
         no_edge_uqe = no_edge[:].rearrange("p j (u q e) -> p j u q e", u=HALF, e=HALF)
         weight_uqe = weight[:].rearrange("p j (u q e) -> p j u q e", u=HALF, e=HALF)
         for j in range(PACK):
-            nc.vector.tensor_scalar(
-                out=no_edge_uqe[:, j],
-                in0=adj_uqe[:, j],
-                scalar1=0.0,
-                scalar2=None,
-                op0=ALU.is_equal,
-                op1=ALU.add,
-                accum_out=n_no_edge[:, j : j + 1],
+            nc.vector.tensor_single_scalar(
+                out=no_edge_uqe[:, j], in_=adj_uqe[:, j], scalar=0.0, op=ALU.is_equal
             )
-            for u in range(HALF):
-                nc.vector.scalar_tensor_tensor(
-                    out=weight_uqe[:, j, u],
-                    in0=adj_uqe[:, j, u],
-                    scalar=INV_SQRT_DIM,
-                    in1=no_edge_uqe[:, j, u],
-                    op0=ALU.mult,
-                    op1=ALU.add,
-                )
             no_edge_ps = psum.tile([P, PACK, P], BF16, tag="emT", bufs=2)
             for b in range(PACK):
                 nc.tensor.transpose(no_edge_ps[:, b, :], no_edge[:, j, block(b)], ident_bf[:])
             nc.scalar.mul(out=no_edge_T[:, j], in_=no_edge_ps[:], mul=NO_EDGE)
-
-        is_feature = const.tile([P, PACK, FEATS], BF16)
-        n_feature = const.tile([P, PACK], F32)
         for j in range(PACK):
-            nc.vector.tensor_scalar(
-                out=is_feature[:, j],
-                in0=x_sb[:, j],
-                scalar1=0.0,
-                scalar2=None,
-                op0=ALU.not_equal,
-                op1=ALU.add,
-                accum_out=n_feature[:, j : j + 1],
-            )
-        has_feature = const.tile([P, PACK], F32)
-        nc.vector.tensor_single_scalar(out=has_feature[:], in_=n_feature[:], scalar=0.0, op=ALU.is_gt)
-        keep = const.tile([P, PACK], F32)
-        nc.vector.scalar_tensor_tensor(
-            out=keep[:],
-            in0=n_no_edge[:],
-            scalar=float(NODES),
-            in1=has_feature[:],
-            op0=ALU.is_lt,
-            op1=ALU.mult,
-        )
+            for u in range(HALF):
+                nc.vector.scalar_tensor_tensor(
+                    out=weight_uqe[:, j, u],
+                    in0=adj_uqe[:, j, u],
+                    scalar=LEAK_OVER_SQRT_DIM,
+                    in1=no_edge_uqe[:, j, u],
+                    op0=ALU.mult,
+                    op1=ALU.add,
+                )
 
+        x_words = x_sb[:].bitcast(F32).rearrange("p t (w u) -> p t u w", u=HALF)
+        x_grouped = const.tile([P, PACK, P, PACK], BF16, align_bytes=64)
+        x_grouped_words = x_grouped[:].bitcast(F32)
         x_codes = const.tile([P, NODES], U32, align_bytes=64)
         x_scales = const.tile([P, NODES], U8, align_bytes=64)
-        nc.vector.quantize_mx(
-            out=x_codes[:].bitcast(FP8X4),
-            scales=x_scales[:],
-            in_=x_grouped[:].rearrange("p t q s -> p (t q s)"),
-        )
+
+        def quantise_x():
+            for first in range(0, PACK, PAIR):
+                xT_ps = psum.tile([P, PAIR, HALF, P], F32, tag="emT", bufs=2)
+                for t in range(PAIR):
+                    for u in range(HALF):
+                        nc.tensor.transpose(xT_ps[:, t, u, :], x_words[:, first + t, u, :], ident_f32[:])
+                nc.scalar.copy(
+                    out=x_grouped_words[:, first : first + PAIR],
+                    in_=xT_ps[:].rearrange("p t u q -> p t q u"),
+                )
+            nc.vector.quantize_mx(
+                out=x_codes[:].bitcast(FP8X4),
+                scales=x_scales[:],
+                in_=x_grouped[:].rearrange("p t q s -> p (t q s)"),
+            )
+
+        x_size = const.tile([P, PACK], F32)
+        has_edge = const.tile([P, PACK], F32)
+        keep = const.tile([P, PACK], F32)
+
+        def measure_x(j):
+            if not 0 <= j < PACK:
+                return
+            x_abs = work.tile([P, FEATS], BF16)
+            nc.scalar.activation(
+                out=x_abs[:], in_=x_sb[:, j], func=ACT.Abs, accum_out=x_size[:, j : j + 1]
+            )
+
+        def find_kept_rows(neg_max):
+            nc.vector.tensor_single_scalar(
+                out=has_edge[:], in_=neg_max[:], scalar=-0.5 * NO_EDGE, op=ALU.is_lt
+            )
+            nc.vector.scalar_tensor_tensor(
+                out=keep[:], in0=x_size[:], scalar=0.0, in1=has_edge[:], op0=ALU.is_gt, op1=ALU.mult
+            )
 
         w_grouped_of = {}
         w_mx_of = {}
@@ -234,6 +241,8 @@ def tile_gatlayersinglebatch_pa_t_kernel(tc, h, a, kernel, f_self, f_other, out)
 
         dense_of = {}
         z_of = {}
+        y_of = {}
+        rise_of = {}
         neg_max_of = {}
         em_of = {}
         den_of = {}
@@ -266,26 +275,56 @@ def tile_gatlayersinglebatch_pa_t_kernel(tc, h, a, kernel, f_self, f_other, out)
             if not 0 <= g < UNITS:
                 return
             if g % PAIR == 0:
-                z = work.tile([P, PAIR, NODES], F32)
+                y = z_of[g // PAIR][:, 1, :]
+            else:
+                z = work.tile([P, PAIR, NODES], F32, bufs=5)
                 z_of[g // PAIR] = z
-            nc.vector.tensor_tensor(
-                out=z_of[g // PAIR][:, g % PAIR, :], in0=dense_of[g][:], in1=weight[:, g % PACK, :], op=ALU.mult
+                y_odd = work.tile([P, NODES], F32)
+                y = y_odd[:]
+            nc.vector.tensor_tensor(out=y, in0=dense_of[g][:], in1=weight[:, g % PACK, :], op=ALU.mult)
+            y_of[g] = y
+
+        def leak_on_vector(g):
+            if not 0 <= g < UNITS:
+                return
+            nc.vector.scalar_tensor_tensor(
+                out=z_of[g // PAIR][:, 0, :],
+                in0=y_of[g],
+                scalar=1.0 / LEAK,
+                in1=y_of[g],
+                op0=ALU.mult,
+                op1=ALU.max,
             )
 
-        def leak(k):
-            if not 0 <= k < PAIRS:
+        def rise(g):
+            if not 0 <= g < UNITS:
                 return
-            z_flat = z_of[k][:].rearrange("p v m -> p (v m)")
-            nc.vector.scalar_tensor_tensor(
-                out=z_flat, in0=z_flat, scalar=LEAK, in1=z_flat, op0=ALU.mult, op1=ALU.max
+            above = work.tile([P, NODES], F32)
+            nc.scalar.activation(out=above[:], in_=y_of[g], func=ACT.Relu, scale=RISE)
+            rise_of[g] = above
+
+        def leak_on_gpsimd(g):
+            if not 0 <= g < UNITS:
+                return
+            nc.gpsimd.tensor_tensor(
+                out=z_of[g // PAIR][:, 1, :], in0=y_of[g], in1=rise_of[g][:], op=ALU.add
             )
 
         def row_max(k):
             if not 0 <= k < PAIRS:
                 return
-            neg_max = work.tile([P, PAIR], F32)
-            nc.vector.tensor_reduce(out=neg_max[:], in_=z_of[k][:], axis=AXIS.X, op=ALU.max, negate=True)
-            neg_max_of[k] = neg_max
+            i = k // PAIRS_PER_HEAD
+            if k % PAIRS_PER_HEAD == 0:
+                neg_max = work.tile([P, PACK], F32)
+                neg_max_of[i] = neg_max
+            first = PAIR * k % PACK
+            nc.vector.tensor_reduce(
+                out=neg_max_of[i][:, first : first + PAIR],
+                in_=z_of[k][:],
+                axis=AXIS.X,
+                op=ALU.max,
+                negate=True,
+            )
 
         def exponentials(k):
             if not 0 <= k < PAIRS:
@@ -300,7 +339,7 @@ def tile_gatlayersinglebatch_pa_t_kernel(tc, h, a, kernel, f_self, f_other, out)
                     out=em[:, v, :],
                     in_=z_of[k][:, v, :],
                     func=ACT.Exp,
-                    bias=neg_max_of[k][:, v : v + 1],
+                    bias=neg_max_of[k // PAIRS_PER_HEAD][:, j : j + 1],
                     scale=1.0,
                     accum_out=den_of[k // PAIRS_PER_HEAD][:, j : j + 1],
                 )
@@ -379,30 +418,37 @@ def tile_gatlayersinglebatch_pa_t_kernel(tc, h, a, kernel, f_self, f_other, out)
             if k % PAIRS_PER_HEAD == PAIRS_PER_HEAD - 1:
                 nc.sync.dma_start(out=out_rows[:, :, block(i)], in_=result_of[i][:])
 
-        for k in range(-2, PAIRS + 3):
-            i = k // PAIRS_PER_HEAD
-            first_of_head = k % PAIRS_PER_HEAD == 0
-            score(PAIR * k + 4)
-            exponentials(k - 1)
-            leak(k)
-            weigh(PAIR * k + 2)
-            multiply(k - 3)
-            if first_of_head:
-                regroup_em(k - 2)
-            else:
-                project(i + 1)
-                copy_f(i + 2)
-                regroup_em(k - 2)
-            transpose_em(k - 1)
-            score(PAIR * k + 5)
-            row_max(k)
-            weigh(PAIR * k + 3)
-            finish(k - 3)
-            quantise_em(k - 2)
-            if first_of_head:
-                row_scales(i - 1)
-                transpose_f(i + 2)
-                regroup_w(i + 1)
-                quantise_w(i + 1)
-                regroup_feats(i)
-                quantise_feats(i)
+        with tc.manual_schedule(engines={mybir.EngineType.DVE, mybir.EngineType.Pool}):
+            for k in range(-2, PAIRS + 5):
+                i = k // PAIRS_PER_HEAD
+                first_of_head = k % PAIRS_PER_HEAD == 0
+                weigh(PAIR * k + 3)
+                finish(k - 5)
+                regroup_em(k - 3)
+                if first_of_head:
+                    regroup_feats(i - 1)
+                rise(PAIR * k + 3)
+                multiply(k - 4)
+                score(PAIR * k + 5)
+                row_max(k - 1)
+                exponentials(k - 2)
+                score(PAIR * k + 4)
+                transpose_em(k - 2)
+                weigh(PAIR * k + 2)
+                quantise_em(k - 3)
+                if k == -1:
+                    quantise_x()
+                measure_x(k + 2)
+                if first_of_head:
+                    if i == 2:
+                        find_kept_rows(neg_max_of[0])
+                    transpose_f(i + 2)
+                    row_scales(i - 2)
+                    quantise_w(i)
+                else:
+                    copy_f(i + 2)
+                    regroup_w(i + 1)
+                    project(i)
+                    quantise_feats(i - 1)
+                leak_on_vector(PAIR * k + 2)
+                leak_on_gpsimd(PAIR * k + 3)

@@ -92,7 +92,7 @@ def tile_gatlayersinglebatch_pa_t_kernel(tc, h, a, kernel, f_self, f_other, out)
         def transpose_f(i):
             if not 0 <= i < HEADS:
                 return
-            fT_ps = psum.tile([P, 2, PACK, P], BF16, tag="fT")
+            fT_ps = psum.tile([P, 2, PACK, P], BF16, tag="head")
             for j in range(PACK):
                 nc.tensor.transpose(fT_ps[:, 0, j, :], fs_sb[:, i, j, :], ident_bf[:])
             for t in range(PACK):
@@ -110,8 +110,9 @@ def tile_gatlayersinglebatch_pa_t_kernel(tc, h, a, kernel, f_self, f_other, out)
             )
             fT_of[i] = fT
 
-        transpose_f(0)
-        copy_f(0)
+        for i in range(2):
+            transpose_f(i)
+            copy_f(i)
 
         no_edge = const.tile([P, PACK, NODES], BF16)
         weight = const.tile([P, PACK, NODES], F32)
@@ -210,7 +211,7 @@ def tile_gatlayersinglebatch_pa_t_kernel(tc, h, a, kernel, f_self, f_other, out)
             if not 0 <= i < HEADS:
                 return
             w_codes, w_scales = w_mx_of[i]
-            feat_ps = psum.tile([P, PACK, OUT], F32, tag="feat")
+            feat_ps = psum.tile([P, PACK, OUT], F32, tag="head")
             for t in range(PACK):
                 nc.tensor.matmul_mx(
                     out=feat_ps[:, t, :],
@@ -258,7 +259,7 @@ def tile_gatlayersinglebatch_pa_t_kernel(tc, h, a, kernel, f_self, f_other, out)
                 return
             fT = fT_of[g // PACK]
             j = g % PACK
-            dense_ps = psum.tile([P, NODES], F32, tag="dense", bufs=3)
+            dense_ps = psum.tile([P, NODES], F32, tag="dense", bufs=4)
             nc.tensor.matmul(out=dense_ps[:], lhsT=fT[:, 0, block(j)], rhs=fT[:, 1, :], start=True, stop=False)
             for b in range(PACK):
                 nc.tensor.matmul(
@@ -271,44 +272,67 @@ def tile_gatlayersinglebatch_pa_t_kernel(tc, h, a, kernel, f_self, f_other, out)
                 )
             dense_of[g] = dense_ps
 
+        def leaks_on_vector(k):
+            return k % 2 == 1
+
         def weigh(g):
             if not 0 <= g < UNITS:
                 return
-            if g % PAIR == 0:
-                y = z_of[g // PAIR][:, 1, :]
+            k = g // PAIR
+            if k not in z_of:
+                z = work.tile([P, PAIR, NODES], F32, bufs=6)
+                z_of[k] = z
+            if not leaks_on_vector(k):
+                y = z_of[k][:, g % PAIR, :]
+            elif g % PAIR == 0:
+                y = z_of[k][:, 1, :]
             else:
-                z = work.tile([P, PAIR, NODES], F32, bufs=5)
-                z_of[g // PAIR] = z
-                y_odd = work.tile([P, NODES], F32)
-                y = y_odd[:]
+                y_second = work.tile([P, NODES], F32)
+                y = y_second[:]
             nc.vector.tensor_tensor(out=y, in0=dense_of[g][:], in1=weight[:, g % PACK, :], op=ALU.mult)
             y_of[g] = y
 
-        def leak_on_vector(g):
-            if not 0 <= g < UNITS:
+        def rise_second(k):
+            if not 0 <= k < PAIRS or not leaks_on_vector(k):
                 return
-            nc.vector.scalar_tensor_tensor(
-                out=z_of[g // PAIR][:, 0, :],
-                in0=y_of[g],
-                scalar=1.0 / LEAK,
-                in1=y_of[g],
-                op0=ALU.mult,
-                op1=ALU.max,
-            )
+            above_second = work.tile([P, NODES], F32)
+            nc.scalar.activation(out=above_second[:], in_=y_of[PAIR * k + 1], func=ACT.Relu, scale=RISE)
+            rise_of[k] = above_second
 
-        def rise(g):
-            if not 0 <= g < UNITS:
+        def leak_or_rise(k):
+            if not 0 <= k < PAIRS:
                 return
-            above = work.tile([P, NODES], F32)
-            nc.scalar.activation(out=above[:], in_=y_of[g], func=ACT.Relu, scale=RISE)
-            rise_of[g] = above
+            if leaks_on_vector(k):
+                nc.vector.scalar_tensor_tensor(
+                    out=z_of[k][:, 0, :],
+                    in0=y_of[PAIR * k],
+                    scalar=1.0 / LEAK,
+                    in1=y_of[PAIR * k],
+                    op0=ALU.mult,
+                    op1=ALU.max,
+                )
+            else:
+                above = work.tile([P, PAIR * NODES], F32)
+                nc.vector.tensor_scalar(
+                    out=above[:],
+                    in0=z_of[k][:].rearrange("p v m -> p (v m)"),
+                    scalar1=RISE,
+                    scalar2=0.0,
+                    op0=ALU.mult,
+                    op1=ALU.max,
+                )
+                rise_of[k] = above
 
-        def leak_on_gpsimd(g):
-            if not 0 <= g < UNITS:
+        def add_rise(k):
+            if not 0 <= k < PAIRS:
                 return
-            nc.gpsimd.tensor_tensor(
-                out=z_of[g // PAIR][:, 1, :], in0=y_of[g], in1=rise_of[g][:], op=ALU.add
-            )
+            if leaks_on_vector(k):
+                nc.gpsimd.tensor_tensor(
+                    out=z_of[k][:, 1, :], in0=y_of[PAIR * k + 1], in1=rise_of[k][:], op=ALU.add
+                )
+            else:
+                z_flat = z_of[k][:].rearrange("p v m -> p (v m)")
+                nc.gpsimd.tensor_tensor(out=z_flat, in0=z_flat, in1=rise_of[k][:], op=ALU.add)
 
         def row_max(k):
             if not 0 <= k < PAIRS:
@@ -330,7 +354,7 @@ def tile_gatlayersinglebatch_pa_t_kernel(tc, h, a, kernel, f_self, f_other, out)
             if not 0 <= k < PAIRS:
                 return
             if k % PAIRS_PER_HEAD == 0:
-                den = work.tile([P, PACK], F32)
+                den = work.tile([P, PACK], F32, bufs=4)
                 den_of[k // PAIRS_PER_HEAD] = den
             em = work.tile([P, PAIR, NODES], BF16)
             for v in range(PAIR):
@@ -418,37 +442,40 @@ def tile_gatlayersinglebatch_pa_t_kernel(tc, h, a, kernel, f_self, f_other, out)
             if k % PAIRS_PER_HEAD == PAIRS_PER_HEAD - 1:
                 nc.sync.dma_start(out=out_rows[:, :, block(i)], in_=result_of[i][:])
 
-        with tc.manual_schedule(engines={mybir.EngineType.DVE, mybir.EngineType.Pool}):
-            for k in range(-2, PAIRS + 5):
+        with tc.manual_schedule():
+            for k in range(-2, PAIRS + 8):
                 i = k // PAIRS_PER_HEAD
                 first_of_head = k % PAIRS_PER_HEAD == 0
-                weigh(PAIR * k + 3)
-                finish(k - 5)
-                regroup_em(k - 3)
+                finish(k - 7)
+                regroup_em(k - 4)
                 if first_of_head:
-                    regroup_feats(i - 1)
-                rise(PAIR * k + 3)
-                multiply(k - 4)
-                score(PAIR * k + 5)
-                row_max(k - 1)
-                exponentials(k - 2)
-                score(PAIR * k + 4)
-                transpose_em(k - 2)
-                weigh(PAIR * k + 2)
-                quantise_em(k - 3)
-                if k == -1:
+                    regroup_feats(i - 2)
+                elif i >= 0:
+                    copy_f(i + 2)
+                transpose_em(k - 3)
+                if k == 1:
                     quantise_x()
-                measure_x(k + 2)
+                score(PAIR * k + 4)
+                score(PAIR * k + 5)
+                multiply(k - 6)
+                if first_of_head and i >= 0:
+                    transpose_f(i + 2)
+                if not first_of_head:
+                    project(i - 1)
+                weigh(PAIR * k + 3)
+                row_max(k - 1)
+                weigh(PAIR * k + 2)
+                rise_second(k + 1)
+                exponentials(k - 2)
+                quantise_em(k - 5)
+                measure_x(k - 1)
                 if first_of_head:
+                    quantise_w(i - 1)
+                else:
+                    regroup_w(i)
+                    quantise_feats(i - 2)
                     if i == 2:
                         find_kept_rows(neg_max_of[0])
-                    transpose_f(i + 2)
                     row_scales(i - 2)
-                    quantise_w(i)
-                else:
-                    copy_f(i + 2)
-                    regroup_w(i + 1)
-                    project(i)
-                    quantise_feats(i - 1)
-                leak_on_vector(PAIR * k + 2)
-                leak_on_gpsimd(PAIR * k + 3)
+                leak_or_rise(k + 1)
+                add_rise(k + 1)

@@ -25,6 +25,7 @@ PAIR = 2
 UNITS = HEADS * PACK
 PAIRS = UNITS // PAIR
 PAIRS_PER_HEAD = PACK // PAIR
+LAST = 3
 LOAD_HEADS = 4
 
 LEAK = 0.2
@@ -145,7 +146,7 @@ def tile_gatlayersinglebatch_pa_t_kernel(tc, h, a, kernel, f_self, f_other, out)
         x_codes = const.tile([P, NODES], U32, align_bytes=64)
         x_scales = const.tile([P, NODES], U8, align_bytes=64)
 
-        def quantise_x():
+        def regroup_x():
             for first in range(0, PACK, PAIR):
                 xT_ps = psum.tile([P, PAIR, HALF, P], F32, tag="emT", bufs=2)
                 for t in range(PAIR):
@@ -155,6 +156,8 @@ def tile_gatlayersinglebatch_pa_t_kernel(tc, h, a, kernel, f_self, f_other, out)
                     out=x_grouped_words[:, first : first + PAIR],
                     in_=xT_ps[:].rearrange("p t u q -> p t q u"),
                 )
+
+        def quantise_x():
             nc.vector.quantize_mx(
                 out=x_codes[:].bitcast(FP8X4),
                 scales=x_scales[:],
@@ -272,67 +275,50 @@ def tile_gatlayersinglebatch_pa_t_kernel(tc, h, a, kernel, f_self, f_other, out)
                 )
             dense_of[g] = dense_ps
 
-        def leaks_on_vector(k):
-            return k % 2 == 1
+        def new_z(k):
+            z = work.tile([P, PAIR, NODES], F32, bufs=6)
+            z_of[k] = z
+
+        new_z(-1)
 
         def weigh(g):
             if not 0 <= g < UNITS:
                 return
             k = g // PAIR
-            if k not in z_of:
-                z = work.tile([P, PAIR, NODES], F32, bufs=6)
-                z_of[k] = z
-            if not leaks_on_vector(k):
-                y = z_of[k][:, g % PAIR, :]
-            elif g % PAIR == 0:
-                y = z_of[k][:, 1, :]
+            if g % PAIR == 0:
+                y = z_of[k - 1][:, 1, :]
             else:
-                y_second = work.tile([P, NODES], F32)
+                y_second = work.tile([P, NODES], F32, bufs=4)
                 y = y_second[:]
             nc.vector.tensor_tensor(out=y, in0=dense_of[g][:], in1=weight[:, g % PACK, :], op=ALU.mult)
             y_of[g] = y
 
+        def leak_first(k):
+            if not 0 <= k < PAIRS:
+                return
+            new_z(k)
+            nc.vector.scalar_tensor_tensor(
+                out=z_of[k][:, 0, :],
+                in0=y_of[PAIR * k],
+                scalar=1.0 / LEAK,
+                in1=y_of[PAIR * k],
+                op0=ALU.mult,
+                op1=ALU.max,
+            )
+
         def rise_second(k):
-            if not 0 <= k < PAIRS or not leaks_on_vector(k):
-                return
-            above_second = work.tile([P, NODES], F32)
-            nc.scalar.activation(out=above_second[:], in_=y_of[PAIR * k + 1], func=ACT.Relu, scale=RISE)
-            rise_of[k] = above_second
-
-        def leak_or_rise(k):
             if not 0 <= k < PAIRS:
                 return
-            if leaks_on_vector(k):
-                nc.vector.scalar_tensor_tensor(
-                    out=z_of[k][:, 0, :],
-                    in0=y_of[PAIR * k],
-                    scalar=1.0 / LEAK,
-                    in1=y_of[PAIR * k],
-                    op0=ALU.mult,
-                    op1=ALU.max,
-                )
-            else:
-                above = work.tile([P, PAIR * NODES], F32)
-                nc.vector.tensor_scalar(
-                    out=above[:],
-                    in0=z_of[k][:].rearrange("p v m -> p (v m)"),
-                    scalar1=RISE,
-                    scalar2=0.0,
-                    op0=ALU.mult,
-                    op1=ALU.max,
-                )
-                rise_of[k] = above
+            above = work.tile([P, NODES], F32)
+            nc.scalar.activation(out=above[:], in_=y_of[PAIR * k + 1], func=ACT.Relu, scale=RISE)
+            rise_of[k] = above
 
-        def add_rise(k):
+        def leak_second(k):
             if not 0 <= k < PAIRS:
                 return
-            if leaks_on_vector(k):
-                nc.gpsimd.tensor_tensor(
-                    out=z_of[k][:, 1, :], in0=y_of[PAIR * k + 1], in1=rise_of[k][:], op=ALU.add
-                )
-            else:
-                z_flat = z_of[k][:].rearrange("p v m -> p (v m)")
-                nc.gpsimd.tensor_tensor(out=z_flat, in0=z_flat, in1=rise_of[k][:], op=ALU.add)
+            nc.gpsimd.tensor_tensor(
+                out=z_of[k][:, 1, :], in0=y_of[PAIR * k + 1], in1=rise_of[k][:], op=ALU.add
+            )
 
         def row_max(k):
             if not 0 <= k < PAIRS:
@@ -391,7 +377,8 @@ def tile_gatlayersinglebatch_pa_t_kernel(tc, h, a, kernel, f_self, f_other, out)
             if not 0 <= k < PAIRS:
                 return
             em_grouped = work.tile([P, PAIR, P, PACK], BF16, align_bytes=64)
-            nc.scalar.copy(out=em_grouped[:].bitcast(F32), in_=emT_of[k][:].rearrange("q v u n -> q v n u"))
+            copy = nc.scalar.copy if k < PAIRS - LAST else nc.vector.tensor_copy
+            copy(out=em_grouped[:].bitcast(F32), in_=emT_of[k][:].rearrange("q v u n -> q v n u"))
             em_grouped_of[k] = em_grouped
 
         def quantise_em(k):
@@ -433,49 +420,61 @@ def tile_gatlayersinglebatch_pa_t_kernel(tc, h, a, kernel, f_self, f_other, out)
                 result_of[i] = result
             for v in range(PAIR):
                 j = (PAIR * k + v) % PACK
-                nc.scalar.activation(
-                    out=result_of[i][:, j, :],
-                    in_=sum_of[k][:, v, :],
-                    func=ACT.Relu,
-                    scale=row_scale_of[i][:, j : j + 1],
-                )
+                if k < PAIRS - LAST:
+                    nc.scalar.activation(
+                        out=result_of[i][:, j, :],
+                        in_=sum_of[k][:, v, :],
+                        func=ACT.Relu,
+                        scale=row_scale_of[i][:, j : j + 1],
+                    )
+                else:
+                    nc.vector.tensor_scalar(
+                        out=result_of[i][:, j, :],
+                        in0=sum_of[k][:, v, :],
+                        scalar1=row_scale_of[i][:, j : j + 1],
+                        scalar2=0.0,
+                        op0=ALU.mult,
+                        op1=ALU.max,
+                    )
             if k % PAIRS_PER_HEAD == PAIRS_PER_HEAD - 1:
                 nc.sync.dma_start(out=out_rows[:, :, block(i)], in_=result_of[i][:])
 
         with tc.manual_schedule():
-            for k in range(-2, PAIRS + 8):
+            for k in range(-2, PAIRS + 7):
                 i = k // PAIRS_PER_HEAD
                 first_of_head = k % PAIRS_PER_HEAD == 0
+                rise_second(k)
                 finish(k - 7)
-                regroup_em(k - 4)
+                regroup_em(k - 5)
                 if first_of_head:
-                    regroup_feats(i - 2)
+                    regroup_feats(i - 1)
                 elif i >= 0:
                     copy_f(i + 2)
-                transpose_em(k - 3)
-                if k == 1:
-                    quantise_x()
+                transpose_em(k - 4)
                 score(PAIR * k + 4)
                 score(PAIR * k + 5)
                 multiply(k - 6)
-                if first_of_head and i >= 0:
-                    transpose_f(i + 2)
+                if k == -1:
+                    regroup_x()
                 if not first_of_head:
-                    project(i - 1)
+                    project(i)
+                elif i >= 0:
+                    transpose_f(i + 2)
                 weigh(PAIR * k + 3)
-                row_max(k - 1)
+                row_max(k - 2)
                 weigh(PAIR * k + 2)
-                rise_second(k + 1)
-                exponentials(k - 2)
-                quantise_em(k - 5)
+                exponentials(k - 3)
                 measure_x(k - 1)
+                quantise_em(k - 5)
+                if k == 0:
+                    quantise_x()
                 if first_of_head:
-                    quantise_w(i - 1)
+                    quantise_w(i)
                 else:
-                    regroup_w(i)
-                    quantise_feats(i - 2)
+                    regroup_w(i + 1)
+                    quantise_feats(i - 1)
                     if i == 2:
                         find_kept_rows(neg_max_of[0])
                     row_scales(i - 2)
-                leak_or_rise(k + 1)
-                add_rise(k + 1)
+                leak_first(k + 1)
+                leak_second(k)

@@ -25,7 +25,10 @@ PAIR = 2
 UNITS = HEADS * PACK
 PAIRS = UNITS // PAIR
 PAIRS_PER_HEAD = PACK // PAIR
-LAST = 3
+SHARE = 384
+REST = NODES - SHARE
+LAST_LEAKS = 2
+LAST = 4
 LOAD_HEADS = 4
 
 LEAK = 0.2
@@ -111,25 +114,25 @@ def tile_gatlayersinglebatch_pa_t_kernel(tc, h, a, kernel, f_self, f_other, out)
             )
             fT_of[i] = fT
 
-        for i in range(2):
-            transpose_f(i)
-            copy_f(i)
-
         no_edge = const.tile([P, PACK, NODES], BF16)
         weight = const.tile([P, PACK, NODES], F32)
         no_edge_T = const.tile([P, PACK, PACK, P], F32)
         adj_uqe = adj_sb[:].rearrange("p j (q u e) -> p j u q e", u=HALF, e=HALF)
         no_edge_uqe = no_edge[:].rearrange("p j (u q e) -> p j u q e", u=HALF, e=HALF)
         weight_uqe = weight[:].rearrange("p j (u q e) -> p j u q e", u=HALF, e=HALF)
-        for j in range(PACK):
+
+        def find_missing_edges(j):
             nc.vector.tensor_single_scalar(
                 out=no_edge_uqe[:, j], in_=adj_uqe[:, j], scalar=0.0, op=ALU.is_equal
             )
-            no_edge_ps = psum.tile([P, PACK, P], BF16, tag="emT", bufs=2)
+
+        def transpose_missing_edges(j):
+            no_edge_ps = psum.tile([P, PACK, P], BF16, tag="dense", bufs=4)
             for b in range(PACK):
                 nc.tensor.transpose(no_edge_ps[:, b, :], no_edge[:, j, block(b)], ident_bf[:])
             nc.scalar.mul(out=no_edge_T[:, j], in_=no_edge_ps[:], mul=NO_EDGE)
-        for j in range(PACK):
+
+        def weights_on_vector(j):
             for u in range(HALF):
                 nc.vector.scalar_tensor_tensor(
                     out=weight_uqe[:, j, u],
@@ -139,6 +142,17 @@ def tile_gatlayersinglebatch_pa_t_kernel(tc, h, a, kernel, f_self, f_other, out)
                     op0=ALU.mult,
                     op1=ALU.add,
                 )
+
+        def weights_on_gpsimd(j):
+            nc.gpsimd.tensor_scalar(
+                out=weight_uqe[:, j],
+                in0=adj_uqe[:, j],
+                scalar1=LEAK_OVER_SQRT_DIM,
+                scalar2=0.0,
+                op0=ALU.mult,
+                op1=ALU.add,
+            )
+            nc.gpsimd.tensor_tensor(out=weight[:, j], in0=weight[:, j], in1=no_edge[:, j], op=ALU.add)
 
         x_words = x_sb[:].bitcast(F32).rearrange("p t (w u) -> p t u w", u=HALF)
         x_grouped = const.tile([P, PACK, P, PACK], BF16, align_bytes=64)
@@ -184,44 +198,56 @@ def tile_gatlayersinglebatch_pa_t_kernel(tc, h, a, kernel, f_self, f_other, out)
                 out=keep[:], in0=x_size[:], scalar=0.0, in1=has_edge[:], op0=ALU.is_gt, op1=ALU.mult
             )
 
-        w_grouped_of = {}
-        w_mx_of = {}
+        grouped_of = {}
+        codes_of = {}
         feat_ps_of = {}
-        feat_grouped_of = {}
-        feat_codes = const.tile([P, HEADS * OUT], U32, align_bytes=64)
-        feat_scales = const.tile([P, HEADS * OUT], U8, align_bytes=64)
 
-        def regroup_w(i):
+        def new_round(r):
+            grouped = work.tile([P, 2, OUT, PACK], BF16, align_bytes=64)
+            grouped_of[r] = grouped
+
+        def regroup_w(i, part):
             if not 0 <= i < HEADS:
                 return
-            w_grouped = work.tile([P, OUT, PACK], BF16, align_bytes=64)
-            nc.scalar.copy(out=w_grouped[:], in_=w_sb[:, i].rearrange("p j o -> p o j"))
-            w_grouped_of[i] = w_grouped
-
-        def quantise_w(i):
-            if not 0 <= i < HEADS:
-                return
-            w_codes = work.tile([P, OUT], U32, align_bytes=64)
-            w_scales = work.tile([P, OUT], U8, align_bytes=64)
-            nc.vector.quantize_mx(
-                out=w_codes[:].bitcast(FP8X4),
-                scales=w_scales[:],
-                in_=w_grouped_of[i][:].rearrange("p o j -> p (o j)"),
+            if part == 0:
+                new_round(i)
+            columns = slice(part * OUT // 2, (part + 1) * OUT // 2)
+            nc.gpsimd.tensor_scalar(
+                out=grouped_of[i][:, 0, columns, :],
+                in0=w_sb[:, i, :, columns].rearrange("p j o -> p o j"),
+                scalar1=1.0,
+                scalar2=0.0,
+                op0=ALU.mult,
+                op1=ALU.add,
             )
-            w_mx_of[i] = (w_codes, w_scales)
+
+        def quantise_round(r):
+            halves = [half for half in range(2) if 0 <= r - 2 * half < HEADS]
+            if not halves:
+                return
+            grouped = slice(halves[0] * OUT * PACK, (halves[-1] + 1) * OUT * PACK)
+            columns = slice(halves[0] * OUT, (halves[-1] + 1) * OUT)
+            codes = work.tile([P, 2 * OUT], U32, align_bytes=64, bufs=4)
+            scales = work.tile([P, 2 * OUT], U8, align_bytes=64, bufs=4)
+            nc.vector.quantize_mx(
+                out=codes[:, columns].bitcast(FP8X4),
+                scales=scales[:, columns],
+                in_=grouped_of[r][:].rearrange("p h o j -> p (h o j)")[:, grouped],
+            )
+            codes_of[r] = (codes, scales)
 
         def project(i):
             if not 0 <= i < HEADS:
                 return
-            w_codes, w_scales = w_mx_of[i]
+            codes, scales = codes_of[i]
             feat_ps = psum.tile([P, PACK, OUT], F32, tag="head")
             for t in range(PACK):
                 nc.tensor.matmul_mx(
                     out=feat_ps[:, t, :],
                     lhsT=x_codes[:, block(t)].bitcast(FP8X4),
                     lhsT_scale=x_scales[:, block(t)],
-                    rhs=w_codes[:].bitcast(FP8X4),
-                    rhs_scale=w_scales[:],
+                    rhs=codes[:, block(0)].bitcast(FP8X4),
+                    rhs_scale=scales[:, block(0)],
                     start=True,
                     stop=True,
                 )
@@ -230,22 +256,12 @@ def tile_gatlayersinglebatch_pa_t_kernel(tc, h, a, kernel, f_self, f_other, out)
         def regroup_feats(i):
             if not 0 <= i < HEADS:
                 return
-            feat_grouped = work.tile([P, OUT, PACK], BF16, align_bytes=64)
-            nc.scalar.copy(out=feat_grouped[:], in_=feat_ps_of[i][:].rearrange("q t o -> q o t"))
-            feat_grouped_of[i] = feat_grouped
-
-        def quantise_feats(i):
-            if not 0 <= i < HEADS:
-                return
-            nc.vector.quantize_mx(
-                out=feat_codes[:, block(i)].bitcast(FP8X4),
-                scales=feat_scales[:, block(i)],
-                in_=feat_grouped_of[i][:].rearrange("q o t -> q (o t)"),
-            )
+            if i + 2 >= HEADS:
+                new_round(i + 2)
+            nc.scalar.copy(out=grouped_of[i + 2][:, 1], in_=feat_ps_of[i][:].rearrange("q t o -> q o t"))
 
         dense_of = {}
         z_of = {}
-        y_of = {}
         rise_of = {}
         neg_max_of = {}
         em_of = {}
@@ -276,49 +292,54 @@ def tile_gatlayersinglebatch_pa_t_kernel(tc, h, a, kernel, f_self, f_other, out)
             dense_of[g] = dense_ps
 
         def new_z(k):
-            z = work.tile([P, PAIR, NODES], F32, bufs=6)
+            z = work.tile([P, PAIR * NODES + REST + NODES], F32, bufs=6)
             z_of[k] = z
 
         new_z(-1)
 
+        def y_on_vector(k):
+            return z_of[k - 1][:, PAIR * NODES - SHARE : PAIR * NODES]
+
+        def y_on_others(k):
+            return z_of[k - 1][:, PAIR * NODES :]
+
         def weigh(g):
             if not 0 <= g < UNITS:
                 return
-            k = g // PAIR
-            if g % PAIR == 0:
-                y = z_of[k - 1][:, 1, :]
-            else:
-                y_second = work.tile([P, NODES], F32, bufs=4)
-                y = y_second[:]
-            nc.vector.tensor_tensor(out=y, in0=dense_of[g][:], in1=weight[:, g % PACK, :], op=ALU.mult)
-            y_of[g] = y
+            first = PAIR * NODES - SHARE + NODES * (g % PAIR)
+            nc.vector.tensor_tensor(
+                out=z_of[g // PAIR - 1][:, first : first + NODES],
+                in0=dense_of[g][:],
+                in1=weight[:, g % PACK, :],
+                op=ALU.mult,
+            )
 
-        def leak_first(k):
+        def leak_on_vector(out, y):
+            nc.vector.scalar_tensor_tensor(
+                out=out, in0=y, scalar=1.0 / LEAK, in1=y, op0=ALU.mult, op1=ALU.max
+            )
+
+        def leak(k):
             if not 0 <= k < PAIRS:
                 return
             new_z(k)
-            nc.vector.scalar_tensor_tensor(
-                out=z_of[k][:, 0, :],
-                in0=y_of[PAIR * k],
-                scalar=1.0 / LEAK,
-                in1=y_of[PAIR * k],
-                op0=ALU.mult,
-                op1=ALU.max,
-            )
+            leak_on_vector(z_of[k][:, :SHARE], y_on_vector(k))
 
-        def rise_second(k):
-            if not 0 <= k < PAIRS:
+        def rise(k):
+            if not 0 <= k < PAIRS - LAST_LEAKS:
                 return
-            above = work.tile([P, NODES], F32)
-            nc.scalar.activation(out=above[:], in_=y_of[PAIR * k + 1], func=ACT.Relu, scale=RISE)
+            above = work.tile([P, REST + NODES], F32)
+            nc.scalar.activation(out=above[:], in_=y_on_others(k), func=ACT.Relu, scale=RISE)
             rise_of[k] = above
 
-        def leak_second(k):
+        def leak_rest(k):
             if not 0 <= k < PAIRS:
                 return
-            nc.gpsimd.tensor_tensor(
-                out=z_of[k][:, 1, :], in0=y_of[PAIR * k + 1], in1=rise_of[k][:], op=ALU.add
-            )
+            z = z_of[k][:, SHARE : PAIR * NODES]
+            if k < PAIRS - LAST_LEAKS:
+                nc.gpsimd.tensor_tensor(out=z, in0=y_on_others(k), in1=rise_of[k][:], op=ALU.add)
+            else:
+                leak_on_vector(z, y_on_others(k))
 
         def row_max(k):
             if not 0 <= k < PAIRS:
@@ -330,7 +351,7 @@ def tile_gatlayersinglebatch_pa_t_kernel(tc, h, a, kernel, f_self, f_other, out)
             first = PAIR * k % PACK
             nc.vector.tensor_reduce(
                 out=neg_max_of[i][:, first : first + PAIR],
-                in_=z_of[k][:],
+                in_=z_of[k][:, : PAIR * NODES].rearrange("p (v m) -> p v m", v=PAIR),
                 axis=AXIS.X,
                 op=ALU.max,
                 negate=True,
@@ -347,7 +368,7 @@ def tile_gatlayersinglebatch_pa_t_kernel(tc, h, a, kernel, f_self, f_other, out)
                 j = (PAIR * k + v) % PACK
                 nc.scalar.activation(
                     out=em[:, v, :],
-                    in_=z_of[k][:, v, :],
+                    in_=z_of[k][:, v * NODES : (v + 1) * NODES],
                     func=ACT.Exp,
                     bias=neg_max_of[k // PAIRS_PER_HEAD][:, j : j + 1],
                     scale=1.0,
@@ -360,7 +381,7 @@ def tile_gatlayersinglebatch_pa_t_kernel(tc, h, a, kernel, f_self, f_other, out)
                 return
             row_scale = work.tile([P, PACK], F32)
             nc.vector.reciprocal(out=row_scale[:], in_=den_of[i][:])
-            nc.vector.tensor_mul(out=row_scale[:], in0=row_scale[:], in1=keep[:])
+            nc.gpsimd.tensor_tensor(out=row_scale[:], in0=row_scale[:], in1=keep[:], op=ALU.mult)
             row_scale_of[i] = row_scale
 
         def transpose_em(k):
@@ -397,15 +418,15 @@ def tile_gatlayersinglebatch_pa_t_kernel(tc, h, a, kernel, f_self, f_other, out)
             if not 0 <= k < PAIRS:
                 return
             em_codes, em_scales = em_mx_of[k]
-            i = k // PAIRS_PER_HEAD
+            codes, scales = codes_of[k // PAIRS_PER_HEAD + 2]
             sum_ps = psum.tile([P, PAIR, OUT], F32, tag="sum")
             for v in range(PAIR):
                 nc.tensor.matmul_mx(
                     out=sum_ps[:, v, :],
                     lhsT=em_codes[:, block(v)].bitcast(FP8X4),
                     lhsT_scale=em_scales[:, block(v)],
-                    rhs=feat_codes[:, block(i)].bitcast(FP8X4),
-                    rhs_scale=feat_scales[:, block(i)],
+                    rhs=codes[:, block(1)].bitcast(FP8X4),
+                    rhs_scale=scales[:, block(1)],
                     start=True,
                     stop=True,
                 )
@@ -440,15 +461,27 @@ def tile_gatlayersinglebatch_pa_t_kernel(tc, h, a, kernel, f_self, f_other, out)
                 nc.sync.dma_start(out=out_rows[:, :, block(i)], in_=result_of[i][:])
 
         with tc.manual_schedule():
+            for j in range(PACK):
+                find_missing_edges(j)
+            transpose_missing_edges(0)
+            transpose_f(0)
+            copy_f(0)
+            for j in range(1, PACK):
+                transpose_missing_edges(j)
+            for j in range(PAIR):
+                weights_on_vector(j)
+            for j in range(PAIR, PACK):
+                weights_on_gpsimd(j)
+            regroup_w(0, 0)
             for k in range(-2, PAIRS + 7):
                 i = k // PAIRS_PER_HEAD
                 first_of_head = k % PAIRS_PER_HEAD == 0
-                rise_second(k)
-                finish(k - 7)
+                rise(k)
                 regroup_em(k - 5)
+                finish(k - 7)
                 if first_of_head:
                     regroup_feats(i - 1)
-                elif i >= 0:
+                else:
                     copy_f(i + 2)
                 transpose_em(k - 4)
                 score(PAIR * k + 4)
@@ -456,10 +489,10 @@ def tile_gatlayersinglebatch_pa_t_kernel(tc, h, a, kernel, f_self, f_other, out)
                 multiply(k - 6)
                 if k == -1:
                     regroup_x()
-                if not first_of_head:
-                    project(i)
-                elif i >= 0:
+                if first_of_head:
                     transpose_f(i + 2)
+                else:
+                    project(i)
                 weigh(PAIR * k + 3)
                 row_max(k - 2)
                 weigh(PAIR * k + 2)
@@ -468,13 +501,13 @@ def tile_gatlayersinglebatch_pa_t_kernel(tc, h, a, kernel, f_self, f_other, out)
                 quantise_em(k - 5)
                 if k == 0:
                     quantise_x()
-                if first_of_head:
-                    quantise_w(i)
-                else:
-                    regroup_w(i + 1)
-                    quantise_feats(i - 1)
+                    quantise_round(0)
+                if not first_of_head:
+                    if i >= 0:
+                        quantise_round(i + 1)
                     if i == 2:
                         find_kept_rows(neg_max_of[0])
                     row_scales(i - 2)
-                leak_first(k + 1)
-                leak_second(k)
+                leak(k + 1)
+                leak_rest(k)
+                regroup_w((k + 3) // 2, 1 - k % 2)

@@ -25,10 +25,11 @@ PAIR = 2
 UNITS = HEADS * PACK
 PAIRS = UNITS // PAIR
 PAIRS_PER_HEAD = PACK // PAIR
-SHARE = 384
+SHARE = 416
 REST = NODES - SHARE
 LAST_LEAKS = 2
-LAST = 4
+LAST_REGROUPS = 4
+LAST_RESULTS = 1
 LOAD_HEADS = 4
 
 LEAK = 0.2
@@ -118,12 +119,12 @@ def tile_gatlayersinglebatch_pa_t_kernel(tc, h, a, kernel, f_self, f_other, out)
         weight = const.tile([P, PACK, NODES], F32)
         no_edge_T = const.tile([P, PACK, PACK, P], F32)
         adj_uqe = adj_sb[:].rearrange("p j (q u e) -> p j u q e", u=HALF, e=HALF)
-        no_edge_uqe = no_edge[:].rearrange("p j (u q e) -> p j u q e", u=HALF, e=HALF)
+        no_edge_uqe = no_edge[:].rearrange("p j (q u e) -> p j u q e", u=HALF, e=HALF)
         weight_uqe = weight[:].rearrange("p j (u q e) -> p j u q e", u=HALF, e=HALF)
 
         def find_missing_edges(j):
             nc.vector.tensor_single_scalar(
-                out=no_edge_uqe[:, j], in_=adj_uqe[:, j], scalar=0.0, op=ALU.is_equal
+                out=no_edge[:, j], in_=adj_sb[:, j], scalar=0.0, op=ALU.is_equal
             )
 
         def transpose_missing_edges(j):
@@ -152,7 +153,9 @@ def tile_gatlayersinglebatch_pa_t_kernel(tc, h, a, kernel, f_self, f_other, out)
                 op0=ALU.mult,
                 op1=ALU.add,
             )
-            nc.gpsimd.tensor_tensor(out=weight[:, j], in0=weight[:, j], in1=no_edge[:, j], op=ALU.add)
+            nc.gpsimd.tensor_tensor(
+                out=weight_uqe[:, j], in0=weight_uqe[:, j], in1=no_edge_uqe[:, j], op=ALU.add
+            )
 
         x_words = x_sb[:].bitcast(F32).rearrange("p t (w u) -> p t u w", u=HALF)
         x_grouped = const.tile([P, PACK, P, PACK], BF16, align_bytes=64)
@@ -271,7 +274,6 @@ def tile_gatlayersinglebatch_pa_t_kernel(tc, h, a, kernel, f_self, f_other, out)
         em_grouped_of = {}
         em_mx_of = {}
         sum_of = {}
-        result_of = {}
 
         def score(g):
             if not 0 <= g < UNITS:
@@ -280,9 +282,10 @@ def tile_gatlayersinglebatch_pa_t_kernel(tc, h, a, kernel, f_self, f_other, out)
             j = g % PACK
             dense_ps = psum.tile([P, NODES], F32, tag="dense", bufs=4)
             nc.tensor.matmul(out=dense_ps[:], lhsT=fT[:, 0, block(j)], rhs=fT[:, 1, :], start=True, stop=False)
+            dense_natural = dense_ps[:].rearrange("n (u q e) -> n q u e", u=HALF, e=HALF)
             for b in range(PACK):
                 nc.tensor.matmul(
-                    out=dense_ps[:, block(b)],
+                    out=dense_natural[:, b * P // PACK : (b + 1) * P // PACK],
                     lhsT=no_edge_T[:, j, b, :],
                     rhs=ident_f32[:],
                     is_transpose=True,
@@ -397,68 +400,71 @@ def tile_gatlayersinglebatch_pa_t_kernel(tc, h, a, kernel, f_self, f_other, out)
         def regroup_em(k):
             if not 0 <= k < PAIRS:
                 return
-            em_grouped = work.tile([P, PAIR, P, PACK], BF16, align_bytes=64)
-            copy = nc.scalar.copy if k < PAIRS - LAST else nc.vector.tensor_copy
-            copy(out=em_grouped[:].bitcast(F32), in_=emT_of[k][:].rearrange("q v u n -> q v n u"))
-            em_grouped_of[k] = em_grouped
+            i = k // PAIRS_PER_HEAD
+            if k % PAIRS_PER_HEAD == 0:
+                em_grouped = work.tile([P, PACK, P, PACK], BF16, align_bytes=64)
+                em_grouped_of[i] = em_grouped
+            first = PAIR * k % PACK
+            copy = nc.scalar.copy if k < PAIRS - LAST_REGROUPS else nc.vector.tensor_copy
+            copy(
+                out=em_grouped_of[i][:, first : first + PAIR].bitcast(F32),
+                in_=emT_of[k][:].rearrange("q v u n -> q v n u"),
+            )
 
-        def quantise_em(k):
-            if not 0 <= k < PAIRS:
+        def quantise_em(i):
+            if not 0 <= i < HEADS:
                 return
-            em_codes = work.tile([P, PAIR * P], U32, align_bytes=64)
-            em_scales = work.tile([P, PAIR * P], U8, align_bytes=64)
+            em_codes = work.tile([P, NODES], U32, align_bytes=64)
+            em_scales = work.tile([P, NODES], U8, align_bytes=64)
             nc.vector.quantize_mx(
                 out=em_codes[:].bitcast(FP8X4),
                 scales=em_scales[:],
-                in_=em_grouped_of[k][:].rearrange("q v n s -> q (v n s)"),
+                in_=em_grouped_of[i][:].rearrange("q j n s -> q (j n s)"),
             )
-            em_mx_of[k] = (em_codes, em_scales)
+            em_mx_of[i] = (em_codes, em_scales)
 
-        def multiply(k):
-            if not 0 <= k < PAIRS:
+        def multiply(i):
+            if not 0 <= i < HEADS:
                 return
-            em_codes, em_scales = em_mx_of[k]
-            codes, scales = codes_of[k // PAIRS_PER_HEAD + 2]
-            sum_ps = psum.tile([P, PAIR, OUT], F32, tag="sum")
-            for v in range(PAIR):
+            em_codes, em_scales = em_mx_of[i]
+            codes, scales = codes_of[i + 2]
+            sum_ps = psum.tile([P, PACK, OUT], F32, tag="sum")
+            for j in range(PACK):
                 nc.tensor.matmul_mx(
-                    out=sum_ps[:, v, :],
-                    lhsT=em_codes[:, block(v)].bitcast(FP8X4),
-                    lhsT_scale=em_scales[:, block(v)],
+                    out=sum_ps[:, j, :],
+                    lhsT=em_codes[:, block(j)].bitcast(FP8X4),
+                    lhsT_scale=em_scales[:, block(j)],
                     rhs=codes[:, block(1)].bitcast(FP8X4),
                     rhs_scale=scales[:, block(1)],
                     start=True,
                     stop=True,
                 )
-            sum_of[k] = sum_ps
+            sum_of[i] = sum_ps
 
-        def finish(k):
-            if not 0 <= k < PAIRS:
+        def finish(i):
+            if not 0 <= i < HEADS:
                 return
-            i = k // PAIRS_PER_HEAD
-            if k % PAIRS_PER_HEAD == 0:
-                result = work.tile([P, PACK, OUT], F32)
-                result_of[i] = result
-            for v in range(PAIR):
-                j = (PAIR * k + v) % PACK
-                if k < PAIRS - LAST:
+            result = work.tile([P, PACK, OUT], F32)
+            for j in range(PACK):
+                if i < HEADS - LAST_RESULTS:
                     nc.scalar.activation(
-                        out=result_of[i][:, j, :],
-                        in_=sum_of[k][:, v, :],
+                        out=result[:, j, :],
+                        in_=sum_of[i][:, j, :],
                         func=ACT.Relu,
                         scale=row_scale_of[i][:, j : j + 1],
                     )
                 else:
                     nc.vector.tensor_scalar(
-                        out=result_of[i][:, j, :],
-                        in0=sum_of[k][:, v, :],
+                        out=result[:, j, :],
+                        in0=sum_of[i][:, j, :],
                         scalar1=row_scale_of[i][:, j : j + 1],
                         scalar2=0.0,
                         op0=ALU.mult,
                         op1=ALU.max,
                     )
-            if k % PAIRS_PER_HEAD == PAIRS_PER_HEAD - 1:
-                nc.sync.dma_start(out=out_rows[:, :, block(i)], in_=result_of[i][:])
+            stores = [slice(0, PACK)] if i < HEADS - 1 else [slice(0, PAIR), slice(PAIR, PACK)]
+            for slots in stores:
+                nc.sync.dma_start(out=out_rows[:, slots, block(i)], in_=result[:, slots])
 
         with tc.manual_schedule():
             for j in range(PACK):
@@ -472,42 +478,40 @@ def tile_gatlayersinglebatch_pa_t_kernel(tc, h, a, kernel, f_self, f_other, out)
                 weights_on_vector(j)
             for j in range(PAIR, PACK):
                 weights_on_gpsimd(j)
-            regroup_w(0, 0)
             for k in range(-2, PAIRS + 7):
                 i = k // PAIRS_PER_HEAD
                 first_of_head = k % PAIRS_PER_HEAD == 0
                 rise(k)
                 regroup_em(k - 5)
-                finish(k - 7)
                 if first_of_head:
-                    regroup_feats(i - 1)
+                    finish(i - 4)
+                    regroup_feats(i - 2)
                 else:
                     copy_f(i + 2)
                 transpose_em(k - 4)
-                score(PAIR * k + 4)
                 score(PAIR * k + 5)
-                multiply(k - 6)
-                if k == -1:
+                score(PAIR * k + 4)
+                if k == 1:
                     regroup_x()
                 if first_of_head:
                     transpose_f(i + 2)
                 else:
-                    project(i)
+                    multiply(i - 3)
+                    project(i - 1)
                 weigh(PAIR * k + 3)
                 row_max(k - 2)
                 weigh(PAIR * k + 2)
                 exponentials(k - 3)
-                measure_x(k - 1)
-                quantise_em(k - 5)
-                if k == 0:
+                measure_x(k + 1)
+                if k == 2:
                     quantise_x()
-                    quantise_round(0)
-                if not first_of_head:
-                    if i >= 0:
-                        quantise_round(i + 1)
+                if first_of_head:
+                    quantise_em(i - 3)
+                else:
+                    quantise_round(i)
                     if i == 2:
                         find_kept_rows(neg_max_of[0])
                     row_scales(i - 2)
                 leak(k + 1)
                 leak_rest(k)
-                regroup_w((k + 3) // 2, 1 - k % 2)
+                regroup_w((k + 1) // 2, 1 - k % 2)

import math
from contextlib import ExitStack

import concourse.mybir as mybir
from concourse.masks import make_identity

F32 = mybir.dt.float32
BF16 = mybir.dt.bfloat16
U32 = mybir.dt.uint32
U8 = mybir.dt.uint8
FP8X4 = mybir.dt.float8_e4m3fn_x4
ALU = mybir.AluOpType
ACT = mybir.ActivationFunctionType
AXIS = mybir.AxisListType

P = 128
PACK = 4
HALF = 2
NODES = 512
FEATS = 512
HEADS = 16
OUT = 128
DIM = 128
PAIR = 2
UNITS = HEADS * PACK
PAIRS = UNITS // PAIR
PAIRS_PER_HEAD = PACK // PAIR
SHARE = 416
REST = NODES - SHARE
LAST_LEAKS = 2
LAST_REGROUPS = 4
LAST_RESULTS = 1
LOAD_HEADS = 4

LEAK = 0.2
NO_EDGE = -(2.0**100)
LEAK_OVER_SQRT_DIM = LEAK / math.sqrt(DIM)
RISE = 1.0 / LEAK - 1.0

FLOPS = 3 * 2 * HEADS * NODES * NODES * 128


def block(i):
    return slice(i * P, (i + 1) * P)


def tile_gatlayersinglebatch_pa_t_kernel(tc, h, a, kernel, f_self, f_other, out):
    nc = tc.nc
    with ExitStack() as ctx:
        const = ctx.enter_context(tc.tile_pool(name="const", bufs=1))
        work = ctx.enter_context(tc.tile_pool(name="work", bufs=3))
        psum = ctx.enter_context(tc.psum_pool(name="psum", bufs=1))

        adj_sb = const.tile([P, PACK, NODES], BF16)
        x_sb = const.tile([P, PACK, FEATS], BF16)
        fs_sb = const.tile([P, HEADS, PACK, DIM], BF16)
        fo_sb = const.tile([P, HEADS, PACK, DIM], BF16)
        w_sb = const.tile([P, HEADS, PACK, OUT], BF16)
        adj_rows = a.rearrange("b (p j) m -> p (b j) m", j=PACK)

        def load_adj(j):
            nc.sync.dma_start(out=adj_sb[:, j], in_=adj_rows[:, j])

        def load_f(heads):
            nc.sync.dma_start(
                out=fs_sb[:, heads], in_=f_self[heads].rearrange("i (p j) d -> p i j d", j=PACK)
            )
            nc.sync.dma_start(
                out=fo_sb[:, heads], in_=f_other[heads].rearrange("i (p j) d -> p i j d", j=PACK)
            )

        def load_w(heads):
            nc.sync.dma_start(
                out=w_sb[:, heads], in_=kernel[heads].rearrange("i (p j) o -> p i j o", j=PACK)
            )

        load_adj(0)
        load_f(slice(0, 1))
        for j in range(1, PACK):
            load_adj(j)
        nc.sync.dma_start(out=x_sb[:], in_=h.rearrange("b (p j) f -> p (b j) f", j=PACK))
        load_f(slice(1, LOAD_HEADS))
        load_w(slice(0, LOAD_HEADS))
        for first in range(LOAD_HEADS, HEADS, LOAD_HEADS):
            load_f(slice(first, first + LOAD_HEADS))
            load_w(slice(first, first + LOAD_HEADS))
        out_rows = out.rearrange("b (p j) c -> p (b j) c", j=PACK)

        ident_bf = const.tile([P, P], BF16)
        make_identity(nc, ident_bf[:])
        ident_f32 = const.tile([P, P], F32)
        make_identity(nc, ident_f32[:])

        fT_ps_of = {}
        fT_of = {}

        def transpose_f(i):
            if not 0 <= i < HEADS:
                return
            fT_ps = psum.tile([P, 2, PACK, P], BF16, tag="head")
            for j in range(PACK):
                nc.tensor.transpose(fT_ps[:, 0, j, :], fs_sb[:, i, j, :], ident_bf[:])
            for t in range(PACK):
                nc.tensor.transpose(fT_ps[:, 1, t, :], fo_sb[:, i, t, :], ident_bf[:])
            fT_ps_of[i] = fT_ps

        def copy_f(i):
            if not 0 <= i < HEADS:
                return
            fT = work.tile([P, 2, NODES], BF16)
            nc.scalar.copy(out=fT[:, 0, :], in_=fT_ps_of[i][:, 0].rearrange("d j p -> d (j p)"))
            nc.scalar.copy(
                out=fT[:, 1, :].rearrange("d (u q e) -> d u q e", u=HALF, e=HALF),
                in_=fT_ps_of[i][:, 1].rearrange("d (u e) q -> d u q e", e=HALF),
            )
            fT_of[i] = fT

        no_edge = const.tile([P, PACK, NODES], BF16)
        weight = const.tile([P, PACK, NODES], F32)
        no_edge_T = const.tile([P, PACK, PACK, P], F32)
        adj_uqe = adj_sb[:].rearrange("p j (q u e) -> p j u q e", u=HALF, e=HALF)
        no_edge_uqe = no_edge[:].rearrange("p j (q u e) -> p j u q e", u=HALF, e=HALF)
        weight_uqe = weight[:].rearrange("p j (u q e) -> p j u q e", u=HALF, e=HALF)

        def find_missing_edges(j):
            nc.vector.tensor_single_scalar(
                out=no_edge[:, j], in_=adj_sb[:, j], scalar=0.0, op=ALU.is_equal
            )

        def transpose_missing_edges(j):
            no_edge_ps = psum.tile([P, PACK, P], BF16, tag="dense", bufs=4)
            for b in range(PACK):
                nc.tensor.transpose(no_edge_ps[:, b, :], no_edge[:, j, block(b)], ident_bf[:])
            nc.scalar.mul(out=no_edge_T[:, j], in_=no_edge_ps[:], mul=NO_EDGE)

        def weights_on_vector(j):
            for u in range(HALF):
                nc.vector.scalar_tensor_tensor(
                    out=weight_uqe[:, j, u],
                    in0=adj_uqe[:, j, u],
                    scalar=LEAK_OVER_SQRT_DIM,
                    in1=no_edge_uqe[:, j, u],
                    op0=ALU.mult,
                    op1=ALU.add,
                )

        def weights_on_gpsimd(j):
            nc.gpsimd.tensor_scalar(
                out=weight_uqe[:, j],
                in0=adj_uqe[:, j],
                scalar1=LEAK_OVER_SQRT_DIM,
                scalar2=0.0,
                op0=ALU.mult,
                op1=ALU.add,
            )
            nc.gpsimd.tensor_tensor(
                out=weight_uqe[:, j], in0=weight_uqe[:, j], in1=no_edge_uqe[:, j], op=ALU.add
            )

        x_words = x_sb[:].bitcast(F32).rearrange("p t (w u) -> p t u w", u=HALF)
        x_grouped = const.tile([P, PACK, P, PACK], BF16, align_bytes=64)
        x_grouped_words = x_grouped[:].bitcast(F32)
        x_codes = const.tile([P, NODES], U32, align_bytes=64)
        x_scales = const.tile([P, NODES], U8, align_bytes=64)

        def regroup_x():
            for first in range(0, PACK, PAIR):
                xT_ps = psum.tile([P, PAIR, HALF, P], F32, tag="emT", bufs=2)
                for t in range(PAIR):
                    for u in range(HALF):
                        nc.tensor.transpose(xT_ps[:, t, u, :], x_words[:, first + t, u, :], ident_f32[:])
                nc.scalar.copy(
                    out=x_grouped_words[:, first : first + PAIR],
                    in_=xT_ps[:].rearrange("p t u q -> p t q u"),
                )

        def quantise_x():
            nc.vector.quantize_mx(
                out=x_codes[:].bitcast(FP8X4),
                scales=x_scales[:],
                in_=x_grouped[:].rearrange("p t q s -> p (t q s)"),
            )

        x_size = const.tile([P, PACK], F32)
        has_edge = const.tile([P, PACK], F32)
        keep = const.tile([P, PACK], F32)

        def measure_x(j):
            if not 0 <= j < PACK:
                return
            x_abs = work.tile([P, FEATS], BF16)
            nc.scalar.activation(
                out=x_abs[:], in_=x_sb[:, j], func=ACT.Abs, accum_out=x_size[:, j : j + 1]
            )

        def find_kept_rows(neg_max):
            nc.vector.tensor_single_scalar(
                out=has_edge[:], in_=neg_max[:], scalar=-0.5 * NO_EDGE, op=ALU.is_lt
            )
            nc.vector.scalar_tensor_tensor(
                out=keep[:], in0=x_size[:], scalar=0.0, in1=has_edge[:], op0=ALU.is_gt, op1=ALU.mult
            )

        grouped_of = {}
        codes_of = {}
        feat_ps_of = {}

        def new_round(r):
            grouped = work.tile([P, 2, OUT, PACK], BF16, align_bytes=64)
            grouped_of[r] = grouped

        def regroup_w(i, part):
            if not 0 <= i < HEADS:
                return
            if part == 0:
                new_round(i)
            columns = slice(part * OUT // 2, (part + 1) * OUT // 2)
            nc.gpsimd.tensor_scalar(
                out=grouped_of[i][:, 0, columns, :],
                in0=w_sb[:, i, :, columns].rearrange("p j o -> p o j"),
                scalar1=1.0,
                scalar2=0.0,
                op0=ALU.mult,
                op1=ALU.add,
            )

        def quantise_round(r):
            halves = [half for half in range(2) if 0 <= r - 2 * half < HEADS]
            if not halves:
                return
            grouped = slice(halves[0] * OUT * PACK, (halves[-1] + 1) * OUT * PACK)
            columns = slice(halves[0] * OUT, (halves[-1] + 1) * OUT)
            codes = work.tile([P, 2 * OUT], U32, align_bytes=64, bufs=4)
            scales = work.tile([P, 2 * OUT], U8, align_bytes=64, bufs=4)
            nc.vector.quantize_mx(
                out=codes[:, columns].bitcast(FP8X4),
                scales=scales[:, columns],
                in_=grouped_of[r][:].rearrange("p h o j -> p (h o j)")[:, grouped],
            )
            codes_of[r] = (codes, scales)

        def project(i):
            if not 0 <= i < HEADS:
                return
            codes, scales = codes_of[i]
            feat_ps = psum.tile([P, PACK, OUT], F32, tag="head")
            for t in range(PACK):
                nc.tensor.matmul_mx(
                    out=feat_ps[:, t, :],
                    lhsT=x_codes[:, block(t)].bitcast(FP8X4),
                    lhsT_scale=x_scales[:, block(t)],
                    rhs=codes[:, block(0)].bitcast(FP8X4),
                    rhs_scale=scales[:, block(0)],
                    start=True,
                    stop=True,
                )
            feat_ps_of[i] = feat_ps

        def regroup_feats(i):
            if not 0 <= i < HEADS:
                return
            if i + 2 >= HEADS:
                new_round(i + 2)
            nc.scalar.copy(out=grouped_of[i + 2][:, 1], in_=feat_ps_of[i][:].rearrange("q t o -> q o t"))

        dense_of = {}
        z_of = {}
        rise_of = {}
        neg_max_of = {}
        em_of = {}
        den_of = {}
        row_scale_of = {}
        emT_of = {}
        em_grouped_of = {}
        em_mx_of = {}
        sum_of = {}

        def score(g):
            if not 0 <= g < UNITS:
                return
            fT = fT_of[g // PACK]
            j = g % PACK
            dense_ps = psum.tile([P, NODES], F32, tag="dense", bufs=4)
            nc.tensor.matmul(out=dense_ps[:], lhsT=fT[:, 0, block(j)], rhs=fT[:, 1, :], start=True, stop=False)
            dense_natural = dense_ps[:].rearrange("n (u q e) -> n q u e", u=HALF, e=HALF)
            for b in range(PACK):
                nc.tensor.matmul(
                    out=dense_natural[:, b * P // PACK : (b + 1) * P // PACK],
                    lhsT=no_edge_T[:, j, b, :],
                    rhs=ident_f32[:],
                    is_transpose=True,
                    start=False,
                    stop=(b == PACK - 1),
                )
            dense_of[g] = dense_ps

        def new_z(k):
            z = work.tile([P, PAIR * NODES + REST + NODES], F32, bufs=6)
            z_of[k] = z

        new_z(-1)

        def y_on_vector(k):
            return z_of[k - 1][:, PAIR * NODES - SHARE : PAIR * NODES]

        def y_on_others(k):
            return z_of[k - 1][:, PAIR * NODES :]

        def weigh(g):
            if not 0 <= g < UNITS:
                return
            first = PAIR * NODES - SHARE + NODES * (g % PAIR)
            nc.vector.tensor_tensor(
                out=z_of[g // PAIR - 1][:, first : first + NODES],
                in0=dense_of[g][:],
                in1=weight[:, g % PACK, :],
                op=ALU.mult,
            )

        def leak_on_vector(out, y):
            nc.vector.scalar_tensor_tensor(
                out=out, in0=y, scalar=1.0 / LEAK, in1=y, op0=ALU.mult, op1=ALU.max
            )

        def leak(k):
            if not 0 <= k < PAIRS:
                return
            new_z(k)
            leak_on_vector(z_of[k][:, :SHARE], y_on_vector(k))

        def rise(k):
            if not 0 <= k < PAIRS - LAST_LEAKS:
                return
            above = work.tile([P, REST + NODES], F32)
            nc.scalar.activation(out=above[:], in_=y_on_others(k), func=ACT.Relu, scale=RISE)
            rise_of[k] = above

        def leak_rest(k):
            if not 0 <= k < PAIRS:
                return
            z = z_of[k][:, SHARE : PAIR * NODES]
            if k < PAIRS - LAST_LEAKS:
                nc.gpsimd.tensor_tensor(out=z, in0=y_on_others(k), in1=rise_of[k][:], op=ALU.add)
            else:
                leak_on_vector(z, y_on_others(k))

        def row_max(k):
            if not 0 <= k < PAIRS:
                return
            i = k // PAIRS_PER_HEAD
            if k % PAIRS_PER_HEAD == 0:
                neg_max = work.tile([P, PACK], F32)
                neg_max_of[i] = neg_max
            first = PAIR * k % PACK
            nc.vector.tensor_reduce(
                out=neg_max_of[i][:, first : first + PAIR],
                in_=z_of[k][:, : PAIR * NODES].rearrange("p (v m) -> p v m", v=PAIR),
                axis=AXIS.X,
                op=ALU.max,
                negate=True,
            )

        def exponentials(k):
            if not 0 <= k < PAIRS:
                return
            if k % PAIRS_PER_HEAD == 0:
                den = work.tile([P, PACK], F32, bufs=4)
                den_of[k // PAIRS_PER_HEAD] = den
            em = work.tile([P, PAIR, NODES], BF16)
            for v in range(PAIR):
                j = (PAIR * k + v) % PACK
                nc.scalar.activation(
                    out=em[:, v, :],
                    in_=z_of[k][:, v * NODES : (v + 1) * NODES],
                    func=ACT.Exp,
                    bias=neg_max_of[k // PAIRS_PER_HEAD][:, j : j + 1],
                    scale=1.0,
                    accum_out=den_of[k // PAIRS_PER_HEAD][:, j : j + 1],
                )
            em_of[k] = em

        def row_scales(i):
            if not 0 <= i < HEADS:
                return
            row_scale = work.tile([P, PACK], F32)
            nc.vector.reciprocal(out=row_scale[:], in_=den_of[i][:])
            nc.gpsimd.tensor_tensor(out=row_scale[:], in0=row_scale[:], in1=keep[:], op=ALU.mult)
            row_scale_of[i] = row_scale

        def transpose_em(k):
            if not 0 <= k < PAIRS:
                return
            em_words = em_of[k][:].bitcast(F32)
            emT_ps = psum.tile([P, PAIR, HALF, P], F32, tag="emT", bufs=2)
            for v in range(PAIR):
                for u in range(HALF):
                    nc.tensor.transpose(emT_ps[:, v, u, :], em_words[:, v, block(u)], ident_f32[:])
            emT_of[k] = emT_ps

        def regroup_em(k):
            if not 0 <= k < PAIRS:
                return
            i = k // PAIRS_PER_HEAD
            if k % PAIRS_PER_HEAD == 0:
                em_grouped = work.tile([P, PACK, P, PACK], BF16, align_bytes=64)
                em_grouped_of[i] = em_grouped
            first = PAIR * k % PACK
            copy = nc.scalar.copy if k < PAIRS - LAST_REGROUPS else nc.vector.tensor_copy
            copy(
                out=em_grouped_of[i][:, first : first + PAIR].bitcast(F32),
                in_=emT_of[k][:].rearrange("q v u n -> q v n u"),
            )

        def quantise_em(i):
            if not 0 <= i < HEADS:
                return
            em_codes = work.tile([P, NODES], U32, align_bytes=64)
            em_scales = work.tile([P, NODES], U8, align_bytes=64)
            nc.vector.quantize_mx(
                out=em_codes[:].bitcast(FP8X4),
                scales=em_scales[:],
                in_=em_grouped_of[i][:].rearrange("q j n s -> q (j n s)"),
            )
            em_mx_of[i] = (em_codes, em_scales)

        def multiply(i):
            if not 0 <= i < HEADS:
                return
            em_codes, em_scales = em_mx_of[i]
            codes, scales = codes_of[i + 2]
            sum_ps = psum.tile([P, PACK, OUT], F32, tag="sum")
            for j in range(PACK):
                nc.tensor.matmul_mx(
                    out=sum_ps[:, j, :],
                    lhsT=em_codes[:, block(j)].bitcast(FP8X4),
                    lhsT_scale=em_scales[:, block(j)],
                    rhs=codes[:, block(1)].bitcast(FP8X4),
                    rhs_scale=scales[:, block(1)],
                    start=True,
                    stop=True,
                )
            sum_of[i] = sum_ps

        def finish(i):
            if not 0 <= i < HEADS:
                return
            result = work.tile([P, PACK, OUT], F32)
            for j in range(PACK):
                if i < HEADS - LAST_RESULTS:
                    nc.scalar.activation(
                        out=result[:, j, :],
                        in_=sum_of[i][:, j, :],
                        func=ACT.Relu,
                        scale=row_scale_of[i][:, j : j + 1],
                    )
                else:
                    nc.vector.tensor_scalar(
                        out=result[:, j, :],
                        in0=sum_of[i][:, j, :],
                        scalar1=row_scale_of[i][:, j : j + 1],
                        scalar2=0.0,
                        op0=ALU.mult,
                        op1=ALU.max,
                    )
            stores = [slice(0, PACK)] if i < HEADS - 1 else [slice(0, PAIR), slice(PAIR, PACK)]
            for slots in stores:
                nc.sync.dma_start(out=out_rows[:, slots, block(i)], in_=result[:, slots])

        with tc.manual_schedule():
            for j in range(PACK):
                find_missing_edges(j)
            transpose_missing_edges(0)
            transpose_f(0)
            copy_f(0)
            for j in range(1, PACK):
                transpose_missing_edges(j)
            for j in range(PAIR):
                weights_on_vector(j)
            for j in range(PAIR, PACK):
                weights_on_gpsimd(j)
            for k in range(-2, PAIRS + 7):
                i = k // PAIRS_PER_HEAD
                first_of_head = k % PAIRS_PER_HEAD == 0
                rise(k)
                regroup_em(k - 5)
                if first_of_head:
                    finish(i - 4)
                    regroup_feats(i - 2)
                else:
                    copy_f(i + 2)
                transpose_em(k - 4)
                score(PAIR * k + 5)
                score(PAIR * k + 4)
                if k == 1:
                    regroup_x()
                if first_of_head:
                    transpose_f(i + 2)
                else:
                    multiply(i - 3)
                    project(i - 1)
                weigh(PAIR * k + 3)
                row_max(k - 2)
                weigh(PAIR * k + 2)
                exponentials(k - 3)
                measure_x(k + 1)
                if k == 2:
                    quantise_x()
                if first_of_head:
                    quantise_em(i - 3)
                else:
                    quantise_round(i)
                    if i == 2:
                        find_kept_rows(neg_max_of[0])
                    row_scales(i - 2)
                leak(k + 1)
                leak_rest(k)
                regroup_w((k + 1) // 2, 1 - k % 2)
